import numpy as np
import ml_dtypes


def mxq(x, axis, fmt="e4m3"):
    dtype, down = {"e4m3": (ml_dtypes.float8_e4m3fn, 7), "e5m2": (ml_dtypes.float8_e5m2, 14)}[fmt]
    v = np.moveaxis(np.asarray(x, np.float32).astype(ml_dtypes.bfloat16).astype(np.float64), axis, -1)
    blocks = v.reshape(v.shape[:-1] + (-1, 32))
    amax = np.abs(blocks).max(-1, keepdims=True)
    byte = np.maximum(np.where(amax > 0, np.frexp(amax)[1] - 1 + 127, 0) - down, 1)
    scale = np.exp2(byte - 127.0)
    codes = (blocks / scale).astype(np.float32).astype(dtype).astype(np.float64)
    return np.moveaxis((codes * scale).reshape(v.shape), -1, axis)


WIDE = False


def mx_kscale(k):
    if not WIDE:
        return np.ones(k)
    levels = np.array([10, -10, 5, -5, 0])
    a = np.random.permutation(np.resize(levels, k // 512 * 4)).reshape(k // 512, 4)
    idx = np.arange(k)
    return np.exp2(a[idx // 512, idx % 128 // 32])


BF16 = ml_dtypes.bfloat16


def bf(x):
    return np.asarray(x, np.float32).astype(BF16)


def f64(x):
    return np.asarray(x).astype(np.float64)


B, C, T, H = 4, 1536, 512, 512
EPS_LN = 1e-5
EPS_STD = 1e-5


def ln_dim1(z, g, b):
    mu = z.mean(axis=1, keepdims=True)
    var = ((z - mu) ** 2).mean(axis=1, keepdims=True)
    return (z - mu) / np.sqrt(var + EPS_LN) * g[None, :, None] + b[None, :, None]


def stats(x, m):
    mean = (m * x).sum(axis=2)
    std = np.sqrt(np.maximum((m * x * x).sum(axis=2) - mean ** 2, EPS_STD))
    return mean, std


def setup_inputs():
    s = mx_kscale(H)
    drop = np.random.randint(B, size=T)
    mask = (np.arange(B)[:, None, None] != drop[None, None, :]) * 1.0
    off = 0.5 * np.random.standard_normal((B, C, 1))
    gain = 0.5 + np.random.random((B, C, 1))
    pad = np.random.standard_normal((B, C, 1)) * (1.0 - mask)
    x = off + gain * np.random.standard_normal((B, C, T)) + pad
    return {"h": bf(np.tanh(np.random.standard_normal((B, H, T))) * s[None, :, None]),
            "x": bf(x),
            "mask": bf(mask),
            "w2": bf(np.random.standard_normal((C, H)) * 3.0 / np.sqrt(H) / s[None, :]),
            "b2": bf(0.1 * np.random.standard_normal(C)),
            "g2": bf(1.0 + 0.1 * np.random.standard_normal(2 * C)),
            "be2": bf(0.1 * np.random.standard_normal(2 * C))}


def reference(h, x, mask, w2, b2, g2, be2):
    x, mask = f64(x), f64(mask)
    alpha = (mxq(f64(w2), 1, "e4m3") @ mxq(f64(h), 1, "e4m3")) + f64(b2)[None, :, None]
    alpha = np.where(mask == 0, -np.inf, alpha)
    e = np.exp(alpha - alpha.max(axis=2, keepdims=True))
    alpha = e / e.sum(axis=2, keepdims=True)
    mean, std = stats(x, alpha)
    out = np.concatenate([mean, std], axis=1)[:, :, None]
    return ln_dim1(out, f64(g2), f64(be2))

@@ -1,0 +1,294 @@
+from contextlib import ExitStack
+
+import concourse.mybir as mybir
+from concourse.masks import make_identity
+
+F32 = mybir.dt.float32
+BF16 = mybir.dt.bfloat16
+U32 = mybir.dt.uint32
+U8 = mybir.dt.uint8
+FP8X4 = mybir.dt.float8_e4m3fn_x4
+ALU = mybir.AluOpType
+ACT = mybir.ActivationFunctionType
+AXIS = mybir.AxisListType
+
+P = 128
+PACK = 4
+B, C, T, H = 4, 1536, 512, 512
+CT = C // P
+TILES = B * CT
+W_PAIRS = CT // 2
+W_PAIRS_AT_START = 2
+H_PARTS = 4
+LOAD_PARTS = 3
+LAG = 2
+EPS_STD = 1e-5
+EPS_LN = 1e-5
+MASKED = 1e30
+
+FLOPS = 2 * B * C * H * T
+
+
+def tile_attentivestatspool_pb_kernel(tc, h, x, mask, w2, b2, g2, be2, out):
+    nc = tc.nc
+    with ExitStack() as ctx:
+        ctx.enter_context(tc.manual_schedule())
+        keep = ctx.enter_context(tc.tile_pool(name="keep", bufs=1))
+        work = ctx.enter_context(tc.tile_pool(name="work", bufs=3))
+        psum_w = ctx.enter_context(tc.psum_pool(name="psum_w", bufs=2))
+        psum_logits = ctx.enter_context(tc.psum_pool(name="psum_logits", bufs=4))
+        psum_norm = ctx.enter_context(tc.psum_pool(name="psum_norm", bufs=1))
+
+        ident = keep.tile([P, P], F32)
+        make_identity(nc, ident[:])
+        ones = keep.tile([P, P], F32)
+        nc.vector.memset(ones[:], 1.0)
+        ones_bf16 = keep.tile([P, P], BF16)
+        nc.vector.memset(ones_bf16[:], 1.0)
+        warm_in = keep.tile([P, 1], F32)
+        warm_out = keep.tile([P, 1], F32)
+        nc.vector.memset(warm_in[:], 0.0)
+        nc.scalar.activation(out=warm_out[:], in_=warm_in[:], func=ACT.Exp)
+
+        h_raw = keep.tile([P, B, PACK, T], BF16)
+        w_raw = keep.tile([P, CT * H], BF16)
+        x_sb = keep.tile([P, B, CT, T], BF16)
+        mask_row = keep.tile([P, B * T], BF16)
+        gain = keep.tile([P, 2, CT], BF16)
+        shift = keep.tile([P, 2, CT], BF16)
+
+        h_view = h.rearrange("b (p v) t -> b p v t", v=PACK)
+        w_view = w2.rearrange("(p j) k -> p (j k)", j=CT)
+        x_view = x.rearrange("b (p j) t -> b p j t", j=CT)
+        per_part = CT // LOAD_PARTS
+
+        def load_x_part(b, part):
+            js = slice(part * per_part, (part + 1) * per_part)
+            nc.sync.dma_start(out=x_sb[:, b, js, :], in_=x_view[b][:, js, :])
+
+        nc.vector.memset(mask_row[:], 0.0)
+        nc.scalar.dma_start(out=mask_row[0:1, :], in_=mask.rearrange("b o t -> o (b t)"))
+        nc.scalar.dma_start(out=gain[:], in_=g2.rearrange("(s p j) -> p s j", s=2, j=CT))
+        nc.scalar.dma_start(out=shift[:], in_=be2.rearrange("(s p j) -> p s j", s=2, j=CT))
+        nc.sync.dma_start(out=h_raw[:, 0], in_=h_view[0])
+        for part in range(LOAD_PARTS):
+            ks = slice(part * per_part * H, (part + 1) * per_part * H)
+            nc.sync.dma_start(out=w_raw[:, ks], in_=w_view[:, ks])
+            load_x_part(0, part)
+        for b in range(1, B):
+            nc.sync.dma_start(out=h_raw[:, b], in_=h_view[b])
+            for part in range(LOAD_PARTS):
+                load_x_part(b, part)
+
+        h_grouped = keep.tile([P, B, T, PACK], BF16, align_bytes=64)
+        h_codes = keep.tile([P, B, T], U32, align_bytes=64)
+        h_scales = keep.tile([P, B, T], U8, align_bytes=64)
+        w_grouped = keep.tile([P, C * PACK], BF16, align_bytes=64)
+        w_codes = keep.tile([P, C], U32, align_bytes=64)
+        w_scales = keep.tile([P, C], U8, align_bytes=64)
+
+        def regroup_h_part(b, part):
+            ts = slice(part * (T // H_PARTS), (part + 1) * (T // H_PARTS))
+            nc.scalar.copy(
+                out=h_grouped[:, b, ts, :], in_=h_raw[:, b, :, ts].rearrange("p v t -> p t v")
+            )
+
+        def quantise_h(b):
+            nc.vector.quantize_mx(
+                out=h_codes[:, b, :].bitcast(FP8X4),
+                scales=h_scales[:, b, :],
+                in_=h_grouped[:, b].rearrange("p t v -> p (t v)"),
+            )
+
+        w_words = w_raw[:].bitcast(F32).rearrange("p (j q u) -> p j u q", j=CT, u=2)
+        w_grouped_words = w_grouped[:].bitcast(F32).rearrange("p (j c u) -> p j c u", j=CT, u=2)
+
+        def transpose_w_pair(pair):
+            turned = psum_w.tile([P, 2, 2, P], F32)
+            for jj in range(2):
+                for u in range(2):
+                    nc.tensor.transpose(turned[:, jj, u, :], w_words[:, 2 * pair + jj, u, :], ident[:])
+            nc.scalar.copy(
+                out=w_grouped_words[:, 2 * pair : 2 * pair + 2, :, :],
+                in_=turned[:].rearrange("p j u c -> p j c u"),
+            )
+
+        def quantise_w_pair(pair):
+            cs = slice(2 * pair * P, (2 * pair + 2) * P)
+            nc.vector.quantize_mx(
+                out=w_codes[:, cs].bitcast(FP8X4),
+                scales=w_scales[:, cs],
+                in_=w_grouped[:, 2 * pair * P * PACK : (2 * pair + 2) * P * PACK],
+            )
+
+        mask_bias = keep.tile([P, B * T], BF16)
+        for b in range(B):
+            ts = slice(b * T, (b + 1) * T)
+            spread = psum_logits.tile([P, T], F32, tag="logits")
+            nc.tensor.matmul(out=spread[:], lhsT=ones_bf16[:], rhs=mask_row[:, ts], start=True, stop=True)
+            nc.vector.tensor_scalar(
+                out=mask_bias[:, ts], in0=spread[:], scalar1=-1.0, scalar2=MASKED, op0=ALU.add, op1=ALU.mult
+            )
+
+        for part in range(H_PARTS):
+            regroup_h_part(0, part)
+        for pair in range(W_PAIRS_AT_START):
+            transpose_w_pair(pair)
+        quantise_h(0)
+        for pair in range(W_PAIRS_AT_START):
+            quantise_w_pair(pair)
+
+        neg_max = keep.tile([P, TILES], F32)
+        sum_e = keep.tile([P, TILES], F32)
+        sum_ex = keep.tile([P, TILES], F32)
+        sum_exx = keep.tile([P, TILES], F32)
+        masked_of = {}
+        e_of = {}
+        ex_of = {}
+
+        def masked_logits(i):
+            b, j = divmod(i, CT)
+            logits = psum_logits.tile([P, T], F32, tag="logits")
+            nc.tensor.matmul_mx(
+                out=logits[:],
+                lhsT=w_codes[:, j * P : (j + 1) * P].bitcast(FP8X4),
+                lhsT_scale=w_scales[:, j * P : (j + 1) * P],
+                rhs=h_codes[:, b, :].bitcast(FP8X4),
+                rhs_scale=h_scales[:, b, :],
+                start=True,
+                stop=True,
+            )
+            masked = work.tile([P, T], F32)
+            nc.vector.tensor_tensor(
+                out=masked[:], in0=logits[:], in1=mask_bias[:, b * T : (b + 1) * T], op=ALU.add
+            )
+            masked_of[i] = masked
+
+        def exponentials(i):
+            nc.vector.tensor_reduce(
+                out=neg_max[:, i : i + 1], in_=masked_of[i][:], axis=AXIS.X, op=ALU.max, negate=True
+            )
+            e = work.tile([P, T], F32)
+            nc.scalar.activation(
+                out=e[:],
+                in_=masked_of[i][:],
+                func=ACT.Exp,
+                bias=neg_max[:, i : i + 1],
+                scale=1.0,
+                accum_out=sum_e[:, i : i + 1],
+            )
+            e_of[i] = e
+
+        def first_moment(i):
+            b, j = divmod(i, CT)
+            ex = work.tile([P, T], F32)
+            nc.vector.scalar_tensor_tensor(
+                out=ex[:],
+                in0=e_of[i][:],
+                scalar=1.0,
+                in1=x_sb[:, b, j, :],
+                op0=ALU.mult,
+                op1=ALU.mult,
+                accum_out=sum_ex[:, i : i + 1],
+            )
+            ex_of[i] = ex
+
+        def second_moment(i):
+            b, j = divmod(i, CT)
+            exx = work.tile([P, T], F32)
+            nc.vector.scalar_tensor_tensor(
+                out=exx[:],
+                in0=ex_of[i][:],
+                scalar=1.0,
+                in1=x_sb[:, b, j, :],
+                op0=ALU.mult,
+                op1=ALU.mult,
+                accum_out=sum_exx[:, i : i + 1],
+            )
+
+        def prepare_ahead(i):
+            b, j = divmod(i, CT)
+            if b == 0:
+                pair = W_PAIRS_AT_START + j // 2
+                if pair < W_PAIRS and j % 2 == 0:
+                    transpose_w_pair(pair)
+                if pair < W_PAIRS and j % 2 == 1:
+                    quantise_w_pair(pair)
+            if b + 1 < B:
+                if j < H_PARTS:
+                    regroup_h_part(b + 1, j)
+                if j == H_PARTS + 1:
+                    quantise_h(b + 1)
+
+        for i in range(TILES + LAG):
+            if i < TILES:
+                masked_logits(i)
+            if i >= LAG:
+                first_moment(i - LAG)
+            if i < TILES:
+                exponentials(i)
+                prepare_ahead(i)
+            if i >= LAG:
+                second_moment(i - LAG)
+
+        nc.scalar.activation(out=warm_out[:], in_=warm_in[:], func=ACT.Sqrt)
+
+        def by_utterance(t):
+            return t[:].rearrange("p (b j) -> p b j", b=B)
+
+        stats = keep.tile([P, B, 2, CT], F32)
+        mean = stats[:, :, 0, :]
+        inv_e = keep.tile([P, TILES], F32)
+        second = keep.tile([P, B, CT], F32)
+        mean_sq = keep.tile([P, B, CT], F32)
+        nc.vector.reciprocal(out=inv_e[:], in_=sum_e[:])
+        nc.vector.tensor_mul(out=mean, in0=by_utterance(sum_ex), in1=by_utterance(inv_e))
+        nc.vector.tensor_mul(out=second[:], in0=by_utterance(sum_exx), in1=by_utterance(inv_e))
+        nc.vector.tensor_mul(out=mean_sq[:], in0=mean, in1=mean)
+        nc.vector.tensor_sub(out=second[:], in0=second[:], in1=mean_sq[:])
+        nc.vector.tensor_scalar_max(out=second[:], in0=second[:], scalar1=EPS_STD)
+        nc.scalar.activation(out=stats[:, :, 1, :], in_=second[:], func=ACT.Sqrt)
+
+        entries = 2 * C
+        width = 2 * CT
+        flat = stats[:].rearrange("p b s j -> p b (s j)")
+
+        def total_over_all(values, name):
+            row = keep.tile([P, B], F32, name="row_" + name)
+            nc.vector.tensor_reduce(out=row[:], in_=values, axis=AXIS.X, op=ALU.add)
+            total = psum_norm.tile([P, B], F32, name="total_" + name)
+            nc.tensor.matmul(out=total[:], lhsT=ones[:], rhs=row[:], start=True, stop=True)
+            return total
+
+        def along_entries(t):
+            return t[:].unsqueeze(2).to_broadcast([P, B, width])
+
+        def along_utterances(t):
+            return t[:].rearrange("p s j -> p (s j)").unsqueeze(1).to_broadcast([P, B, width])
+
+        mu = keep.tile([P, B], F32)
+        centred = keep.tile([P, B, width], F32)
+        squared = keep.tile([P, B, width], F32)
+        spread = keep.tile([P, B], F32)
+        nc.vector.tensor_scalar_mul(out=mu[:], in0=total_over_all(flat, "v")[:], scalar1=1.0 / entries)
+        nc.vector.tensor_sub(out=centred[:], in0=flat, in1=along_entries(mu))
+        nc.vector.tensor_mul(out=squared[:], in0=centred[:], in1=centred[:])
+        nc.vector.tensor_scalar(
+            out=spread[:],
+            in0=total_over_all(squared[:], "sq")[:],
+            scalar1=1.0 / entries,
+            scalar2=EPS_LN,
+            op0=ALU.mult,
+            op1=ALU.add,
+        )
+        nc.scalar.activation(out=spread[:], in_=spread[:], func=ACT.Sqrt)
+        nc.vector.reciprocal(out=spread[:], in_=spread[:])
+        nc.vector.tensor_mul(out=centred[:], in0=centred[:], in1=along_entries(spread))
+        nc.vector.tensor_mul(out=centred[:], in0=centred[:], in1=along_utterances(gain))
+        nc.vector.tensor_add(out=centred[:], in0=centred[:], in1=along_utterances(shift))
+
+        out_view = out.rearrange("b (s p j) o -> b p s (j o)", s=2, j=CT)
+        for b in range(B):
+            nc.sync.dma_start(
+                out=out_view[b], in_=centred[:, b, :].rearrange("p (s j) -> p s j", s=2)
+            )

@@ -67,7 +67,7 @@ def tile_attentivestatspool_pb_kernel(tc, h, x, mask, w2, b2, g2, be2, out):
             nc.sync.dma_start(out=x_sb[:, b, js, :], in_=x_view[b][:, js, :])
 
         nc.vector.memset(mask_row[:], 0.0)
-        nc.scalar.dma_start(out=mask_row[0:1, :], in_=mask.rearrange("b o t -> o (b t)"))
+        nc.sync.dma_start(out=mask_row[0:1, :], in_=mask.rearrange("b o t -> o (b t)"))
         nc.scalar.dma_start(out=gain[:], in_=g2.rearrange("(s p j) -> p s j", s=2, j=CT))
         nc.scalar.dma_start(out=shift[:], in_=be2.rearrange("(s p j) -> p s j", s=2, j=CT))
         nc.sync.dma_start(out=h_raw[:, 0], in_=h_view[0])
@@ -145,6 +145,7 @@ def tile_attentivestatspool_pb_kernel(tc, h, x, mask, w2, b2, g2, be2, out):
         masked_of = {}
         e_of = {}
         ex_of = {}
+        exx_of = {}
 
         def masked_logits(i):
             b, j = divmod(i, CT)
@@ -196,14 +197,12 @@ def tile_attentivestatspool_pb_kernel(tc, h, x, mask, w2, b2, g2, be2, out):
         def second_moment(i):
             b, j = divmod(i, CT)
             exx = work.tile([P, T], F32)
-            nc.vector.scalar_tensor_tensor(
-                out=exx[:],
-                in0=ex_of[i][:],
-                scalar=1.0,
-                in1=x_sb[:, b, j, :],
-                op0=ALU.mult,
-                op1=ALU.mult,
-                accum_out=sum_exx[:, i : i + 1],
+            nc.gpsimd.tensor_tensor(out=exx[:], in0=ex_of[i][:], in1=x_sb[:, b, j, :], op=ALU.mult)
+            exx_of[i] = exx
+
+        def sum_second_moment(i):
+            nc.scalar.activation(
+                out=exx_of[i][:], in_=exx_of[i][:], func=ACT.Copy, accum_out=sum_exx[:, i : i + 1]
             )
 
         def prepare_ahead(i):
@@ -220,16 +219,18 @@ def tile_attentivestatspool_pb_kernel(tc, h, x, mask, w2, b2, g2, be2, out):
                 if j == H_PARTS + 1:
                     quantise_h(b + 1)
 
-        for i in range(TILES + LAG):
+        for i in range(TILES + LAG + 1):
             if i < TILES:
                 masked_logits(i)
-            if i >= LAG:
+            if LAG <= i < TILES + LAG:
                 first_moment(i - LAG)
+                second_moment(i - LAG)
             if i < TILES:
                 exponentials(i)
+            if i > LAG:
+                sum_second_moment(i - LAG - 1)
+            if i < TILES:
                 prepare_ahead(i)
-            if i >= LAG:
-                second_moment(i - LAG)
 
         nc.scalar.activation(out=warm_out[:], in_=warm_in[:], func=ACT.Sqrt)
 

@@ -16,12 +16,18 @@ P = 128
 PACK = 4
 B, C, T, H = 4, 1536, 512, 512
 CT = C // P
+FT = T // P
+WIDE = 512
+GROUP = WIDE // P
 TILES = B * CT
 W_PAIRS = CT // 2
-W_PAIRS_AT_START = 2
+W_PAIRS_AT_START = GROUP // 2
 H_PARTS = 4
+H_FIRST_ROUND = 5
 LOAD_PARTS = 3
-LAG = 2
+TURN_LAG = GROUP
+EXP_LAG = TURN_LAG + 1
+SUM_LAG = EXP_LAG + 2
 EPS_STD = 1e-5
 EPS_LN = 1e-5
 MASKED = 1e30
@@ -35,25 +41,23 @@ def tile_attentivestatspool_pb_kernel(tc, h, x, mask, w2, b2, g2, be2, out):
         ctx.enter_context(tc.manual_schedule())
         keep = ctx.enter_context(tc.tile_pool(name="keep", bufs=1))
         work = ctx.enter_context(tc.tile_pool(name="work", bufs=3))
-        psum_w = ctx.enter_context(tc.psum_pool(name="psum_w", bufs=2))
-        psum_logits = ctx.enter_context(tc.psum_pool(name="psum_logits", bufs=4))
-        psum_norm = ctx.enter_context(tc.psum_pool(name="psum_norm", bufs=1))
+        psum_t = ctx.enter_context(tc.psum_pool(name="psum_t", bufs=2))
+        psum_c = ctx.enter_context(tc.psum_pool(name="psum_c", bufs=3))
+        psum_small = ctx.enter_context(tc.psum_pool(name="psum_small", bufs=1))
 
         ident = keep.tile([P, P], F32)
         make_identity(nc, ident[:])
         ones = keep.tile([P, P], F32)
         nc.vector.memset(ones[:], 1.0)
-        ones_bf16 = keep.tile([P, P], BF16)
-        nc.vector.memset(ones_bf16[:], 1.0)
         warm_in = keep.tile([P, 1], F32)
         warm_out = keep.tile([P, 1], F32)
         nc.vector.memset(warm_in[:], 0.0)
         nc.scalar.activation(out=warm_out[:], in_=warm_in[:], func=ACT.Exp)
 
+        mask_rows = keep.tile([P, P], BF16)
         h_raw = keep.tile([P, B, PACK, T], BF16)
         w_raw = keep.tile([P, CT * H], BF16)
         x_sb = keep.tile([P, B, CT, T], BF16)
-        mask_row = keep.tile([P, B * T], BF16)
         gain = keep.tile([P, 2, CT], BF16)
         shift = keep.tile([P, 2, CT], BF16)
 
@@ -62,23 +66,30 @@ def tile_attentivestatspool_pb_kernel(tc, h, x, mask, w2, b2, g2, be2, out):
         x_view = x.rearrange("b (p j) t -> b p j t", j=CT)
         per_part = CT // LOAD_PARTS
 
-        def load_x_part(b, part):
-            js = slice(part * per_part, (part + 1) * per_part)
-            nc.sync.dma_start(out=x_sb[:, b, js, :], in_=x_view[b][:, js, :])
-
-        nc.vector.memset(mask_row[:], 0.0)
-        nc.sync.dma_start(out=mask_row[0:1, :], in_=mask.rearrange("b o t -> o (b t)"))
+        nc.vector.memset(mask_rows[:], 0.0)
+        nc.sync.dma_start(
+            out=mask_rows[0 : B * FT, :], in_=mask.rearrange("b o (f t) -> (b o f) t", t=P)
+        )
         nc.scalar.dma_start(out=gain[:], in_=g2.rearrange("(s p j) -> p s j", s=2, j=CT))
         nc.scalar.dma_start(out=shift[:], in_=be2.rearrange("(s p j) -> p s j", s=2, j=CT))
-        nc.sync.dma_start(out=h_raw[:, 0], in_=h_view[0])
-        for part in range(LOAD_PARTS):
-            ks = slice(part * per_part * H, (part + 1) * per_part * H)
-            nc.sync.dma_start(out=w_raw[:, ks], in_=w_view[:, ks])
-            load_x_part(0, part)
-        for b in range(1, B):
+        for b in range(B):
             nc.sync.dma_start(out=h_raw[:, b], in_=h_view[b])
+            if b == 0:
+                for part in range(LOAD_PARTS):
+                    ks = slice(part * per_part * H, (part + 1) * per_part * H)
+                    nc.sync.dma_start(out=w_raw[:, ks], in_=w_view[:, ks])
             for part in range(LOAD_PARTS):
-                load_x_part(b, part)
+                js = slice(part * per_part, (part + 1) * per_part)
+                nc.sync.dma_start(out=x_sb[:, b, js, :], in_=x_view[b][:, js, :])
+
+        bias_rows = keep.tile([P, P], F32)
+        nc.vector.tensor_scalar(
+            out=bias_rows[:], in0=mask_rows[:], scalar1=-1.0, scalar2=MASKED, op0=ALU.add, op1=ALU.mult
+        )
+        bias_turned = psum_small.tile([P, P], F32)
+        nc.tensor.transpose(bias_turned[:], bias_rows[:], ident[:])
+        mask_bias = keep.tile([P, B * FT], F32)
+        nc.vector.tensor_copy(out=mask_bias[:], in_=bias_turned[:, 0 : B * FT])
 
         h_grouped = keep.tile([P, B, T, PACK], BF16, align_bytes=64)
         h_codes = keep.tile([P, B, T], U32, align_bytes=64)
@@ -103,8 +114,8 @@ def tile_attentivestatspool_pb_kernel(tc, h, x, mask, w2, b2, g2, be2, out):
         w_words = w_raw[:].bitcast(F32).rearrange("p (j q u) -> p j u q", j=CT, u=2)
         w_grouped_words = w_grouped[:].bitcast(F32).rearrange("p (j c u) -> p j c u", j=CT, u=2)
 
-        def transpose_w_pair(pair):
-            turned = psum_w.tile([P, 2, 2, P], F32)
+        def prepare_w_pair(pair):
+            turned = psum_t.tile([P, 2, 2, P], F32, tag="logits_t")
             for jj in range(2):
                 for u in range(2):
                     nc.tensor.transpose(turned[:, jj, u, :], w_words[:, 2 * pair + jj, u, :], ident[:])
@@ -112,8 +123,6 @@ def tile_attentivestatspool_pb_kernel(tc, h, x, mask, w2, b2, g2, be2, out):
                 out=w_grouped_words[:, 2 * pair : 2 * pair + 2, :, :],
                 in_=turned[:].rearrange("p j u c -> p j c u"),
             )
-
-        def quantise_w_pair(pair):
             cs = slice(2 * pair * P, (2 * pair + 2) * P)
             nc.vector.quantize_mx(
                 out=w_codes[:, cs].bitcast(FP8X4),
@@ -121,58 +130,64 @@ def tile_attentivestatspool_pb_kernel(tc, h, x, mask, w2, b2, g2, be2, out):
                 in_=w_grouped[:, 2 * pair * P * PACK : (2 * pair + 2) * P * PACK],
             )
 
-        mask_bias = keep.tile([P, B * T], BF16)
-        for b in range(B):
-            ts = slice(b * T, (b + 1) * T)
-            spread = psum_logits.tile([P, T], F32, tag="logits")
-            nc.tensor.matmul(out=spread[:], lhsT=ones_bf16[:], rhs=mask_row[:, ts], start=True, stop=True)
-            nc.vector.tensor_scalar(
-                out=mask_bias[:, ts], in0=spread[:], scalar1=-1.0, scalar2=MASKED, op0=ALU.add, op1=ALU.mult
-            )
-
         for part in range(H_PARTS):
             regroup_h_part(0, part)
-        for pair in range(W_PAIRS_AT_START):
-            transpose_w_pair(pair)
         quantise_h(0)
         for pair in range(W_PAIRS_AT_START):
-            quantise_w_pair(pair)
+            prepare_w_pair(pair)
 
         neg_max = keep.tile([P, TILES], F32)
         sum_e = keep.tile([P, TILES], F32)
         sum_ex = keep.tile([P, TILES], F32)
         sum_exx = keep.tile([P, TILES], F32)
-        masked_of = {}
+        masked_t_of = {}
+        logits_of = {}
         e_of = {}
         ex_of = {}
-        exx_of = {}
 
-        def masked_logits(i):
-            b, j = divmod(i, CT)
-            logits = psum_logits.tile([P, T], F32, tag="logits")
+        def masked_logits_by_frame(n):
+            b, rest = divmod(n, CT)
+            g, f = divmod(rest, FT)
+            logits_t = psum_t.tile([P, WIDE], F32, tag="logits_t")
             nc.tensor.matmul_mx(
-                out=logits[:],
-                lhsT=w_codes[:, j * P : (j + 1) * P].bitcast(FP8X4),
-                lhsT_scale=w_scales[:, j * P : (j + 1) * P],
-                rhs=h_codes[:, b, :].bitcast(FP8X4),
-                rhs_scale=h_scales[:, b, :],
+                out=logits_t[:],
+                lhsT=h_codes[:, b, f * P : (f + 1) * P].bitcast(FP8X4),
+                lhsT_scale=h_scales[:, b, f * P : (f + 1) * P],
+                rhs=w_codes[:, g * WIDE : (g + 1) * WIDE].bitcast(FP8X4),
+                rhs_scale=w_scales[:, g * WIDE : (g + 1) * WIDE],
                 start=True,
                 stop=True,
             )
-            masked = work.tile([P, T], F32)
-            nc.vector.tensor_tensor(
-                out=masked[:], in0=logits[:], in1=mask_bias[:, b * T : (b + 1) * T], op=ALU.add
+            if f == 0:
+                masked_t = work.tile([P, FT, WIDE], F32)
+                masked_t_of[n // FT] = masked_t
+            nc.scalar.activation(
+                out=masked_t_of[n // FT][:, f, :],
+                in_=logits_t[:],
+                func=ACT.Identity,
+                bias=mask_bias[:, b * FT + f : b * FT + f + 1],
+                scale=1.0,
             )
-            masked_of[i] = masked
+
+        def turn_back(i):
+            group, jj = divmod(i, GROUP)
+            logits = psum_c.tile([P, T], F32)
+            for f in range(FT):
+                nc.tensor.transpose(
+                    logits[:, f * P : (f + 1) * P],
+                    masked_t_of[group][:, f, jj * P : (jj + 1) * P],
+                    ident[:],
+                )
+            logits_of[i] = logits
 
         def exponentials(i):
             nc.vector.tensor_reduce(
-                out=neg_max[:, i : i + 1], in_=masked_of[i][:], axis=AXIS.X, op=ALU.max, negate=True
+                out=neg_max[:, i : i + 1], in_=logits_of[i][:], axis=AXIS.X, op=ALU.max, negate=True
             )
             e = work.tile([P, T], F32)
             nc.scalar.activation(
                 out=e[:],
-                in_=masked_of[i][:],
+                in_=logits_of[i][:],
                 func=ACT.Exp,
                 bias=neg_max[:, i : i + 1],
                 scale=1.0,
@@ -197,40 +212,39 @@ def tile_attentivestatspool_pb_kernel(tc, h, x, mask, w2, b2, g2, be2, out):
         def second_moment(i):
             b, j = divmod(i, CT)
             exx = work.tile([P, T], F32)
-            nc.gpsimd.tensor_tensor(out=exx[:], in0=ex_of[i][:], in1=x_sb[:, b, j, :], op=ALU.mult)
-            exx_of[i] = exx
-
-        def sum_second_moment(i):
-            nc.scalar.activation(
-                out=exx_of[i][:], in_=exx_of[i][:], func=ACT.Copy, accum_out=sum_exx[:, i : i + 1]
+            nc.vector.scalar_tensor_tensor(
+                out=exx[:],
+                in0=ex_of[i][:],
+                scalar=1.0,
+                in1=x_sb[:, b, j, :],
+                op0=ALU.mult,
+                op1=ALU.mult,
+                accum_out=sum_exx[:, i : i + 1],
             )
 
-        def prepare_ahead(i):
-            b, j = divmod(i, CT)
-            if b == 0:
-                pair = W_PAIRS_AT_START + j // 2
-                if pair < W_PAIRS and j % 2 == 0:
-                    transpose_w_pair(pair)
-                if pair < W_PAIRS and j % 2 == 1:
-                    quantise_w_pair(pair)
+        def prepare_ahead(n):
+            if W_PAIRS_AT_START + n < W_PAIRS:
+                prepare_w_pair(W_PAIRS_AT_START + n)
+            b, rest = divmod(n, CT)
             if b + 1 < B:
-                if j < H_PARTS:
-                    regroup_h_part(b + 1, j)
-                if j == H_PARTS + 1:
+                if H_FIRST_ROUND <= rest < H_FIRST_ROUND + H_PARTS:
+                    regroup_h_part(b + 1, rest - H_FIRST_ROUND)
+                if rest == H_FIRST_ROUND + H_PARTS + 1:
                     quantise_h(b + 1)
 
-        for i in range(TILES + LAG + 1):
-            if i < TILES:
-                masked_logits(i)
-            if LAG <= i < TILES + LAG:
-                first_moment(i - LAG)
-                second_moment(i - LAG)
-            if i < TILES:
-                exponentials(i)
-            if i > LAG:
-                sum_second_moment(i - LAG - 1)
-            if i < TILES:
-                prepare_ahead(i)
+        for n in range(TILES + SUM_LAG):
+            if n < TILES:
+                masked_logits_by_frame(n)
+            if TURN_LAG <= n < TILES + TURN_LAG:
+                turn_back(n - TURN_LAG)
+            if n >= SUM_LAG:
+                first_moment(n - SUM_LAG)
+            if EXP_LAG <= n < TILES + EXP_LAG:
+                exponentials(n - EXP_LAG)
+            if n >= SUM_LAG:
+                second_moment(n - SUM_LAG)
+            if n < TILES:
+                prepare_ahead(n)
 
         nc.scalar.activation(out=warm_out[:], in_=warm_in[:], func=ACT.Sqrt)
 
@@ -257,7 +271,7 @@ def tile_attentivestatspool_pb_kernel(tc, h, x, mask, w2, b2, g2, be2, out):
         def total_over_all(values, name):
             row = keep.tile([P, B], F32, name="row_" + name)
             nc.vector.tensor_reduce(out=row[:], in_=values, axis=AXIS.X, op=ALU.add)
-            total = psum_norm.tile([P, B], F32, name="total_" + name)
+            total = psum_small.tile([P, B], F32, name="total_" + name)
             nc.tensor.matmul(out=total[:], lhsT=ones[:], rhs=row[:], start=True, stop=True)
             return total
 

@@ -144,6 +144,7 @@ def tile_attentivestatspool_pb_kernel(tc, h, x, mask, w2, b2, g2, be2, out):
         logits_of = {}
         e_of = {}
         ex_of = {}
+        exx_of = {}
 
         def masked_logits_by_frame(n):
             b, rest = divmod(n, CT)
@@ -212,14 +213,12 @@ def tile_attentivestatspool_pb_kernel(tc, h, x, mask, w2, b2, g2, be2, out):
         def second_moment(i):
             b, j = divmod(i, CT)
             exx = work.tile([P, T], F32)
-            nc.vector.scalar_tensor_tensor(
-                out=exx[:],
-                in0=ex_of[i][:],
-                scalar=1.0,
-                in1=x_sb[:, b, j, :],
-                op0=ALU.mult,
-                op1=ALU.mult,
-                accum_out=sum_exx[:, i : i + 1],
+            nc.vector.tensor_tensor(out=exx[:], in0=ex_of[i][:], in1=x_sb[:, b, j, :], op=ALU.mult)
+            exx_of[i] = exx
+
+        def sum_second_moment(i):
+            nc.scalar.activation(
+                out=exx_of[i][:], in_=exx_of[i][:], func=ACT.Copy, accum_out=sum_exx[:, i : i + 1]
             )
 
         def prepare_ahead(n):
@@ -232,17 +231,19 @@ def tile_attentivestatspool_pb_kernel(tc, h, x, mask, w2, b2, g2, be2, out):
                 if rest == H_FIRST_ROUND + H_PARTS + 1:
                     quantise_h(b + 1)
 
-        for n in range(TILES + SUM_LAG):
+        for n in range(TILES + SUM_LAG + 1):
             if n < TILES:
                 masked_logits_by_frame(n)
             if TURN_LAG <= n < TILES + TURN_LAG:
                 turn_back(n - TURN_LAG)
-            if n >= SUM_LAG:
+            if SUM_LAG <= n < TILES + SUM_LAG:
                 first_moment(n - SUM_LAG)
             if EXP_LAG <= n < TILES + EXP_LAG:
                 exponentials(n - EXP_LAG)
-            if n >= SUM_LAG:
+            if SUM_LAG <= n < TILES + SUM_LAG:
                 second_moment(n - SUM_LAG)
+            if n > SUM_LAG:
+                sum_second_moment(n - SUM_LAG - 1)
             if n < TILES:
                 prepare_ahead(n)
 

@@ -20,14 +20,11 @@ FT = T // P
 WIDE = 512
 GROUP = WIDE // P
 TILES = B * CT
+GROUPS = TILES // GROUP
+GROUPS_PER_B = CT // GROUP
 W_PAIRS = CT // 2
-W_PAIRS_AT_START = GROUP // 2
 H_PARTS = 4
-H_FIRST_ROUND = 5
 LOAD_PARTS = 3
-TURN_LAG = GROUP
-EXP_LAG = TURN_LAG + 1
-SUM_LAG = EXP_LAG + 2
 EPS_STD = 1e-5
 EPS_LN = 1e-5
 MASKED = 1e30
@@ -40,10 +37,12 @@ def tile_attentivestatspool_pb_kernel(tc, h, x, mask, w2, b2, g2, be2, out):
     with ExitStack() as ctx:
         ctx.enter_context(tc.manual_schedule())
         keep = ctx.enter_context(tc.tile_pool(name="keep", bufs=1))
-        work = ctx.enter_context(tc.tile_pool(name="work", bufs=3))
-        psum_t = ctx.enter_context(tc.psum_pool(name="psum_t", bufs=2))
-        psum_c = ctx.enter_context(tc.psum_pool(name="psum_c", bufs=3))
-        psum_small = ctx.enter_context(tc.psum_pool(name="psum_small", bufs=1))
+        masked_pool = ctx.enter_context(tc.tile_pool(name="masked_pool", bufs=3))
+        e_pool = ctx.enter_context(tc.tile_pool(name="e_pool", bufs=6))
+        ex_pool = ctx.enter_context(tc.tile_pool(name="ex_pool", bufs=3))
+        junk_pool = ctx.enter_context(tc.tile_pool(name="junk_pool", bufs=2))
+        psum_t = ctx.enter_context(tc.psum_pool(name="psum_t", bufs=4))
+        psum_c = ctx.enter_context(tc.psum_pool(name="psum_c", bufs=4))
 
         ident = keep.tile([P, P], F32)
         make_identity(nc, ident[:])
@@ -66,27 +65,41 @@ def tile_attentivestatspool_pb_kernel(tc, h, x, mask, w2, b2, g2, be2, out):
         x_view = x.rearrange("b (p j) t -> b p j t", j=CT)
         per_part = CT // LOAD_PARTS
 
+        def load_w(part):
+            ks = slice(part * per_part * H, (part + 1) * per_part * H)
+            nc.sync.dma_start(out=w_raw[:, ks], in_=w_view[:, ks])
+
+        def load_h(b):
+            nc.sync.dma_start(out=h_raw[:, b], in_=h_view[b])
+
+        def load_x(b):
+            for part in range(LOAD_PARTS):
+                js = slice(part * per_part, (part + 1) * per_part)
+                nc.sync.dma_start(out=x_sb[:, b, js, :], in_=x_view[b][:, js, :])
+
         nc.vector.memset(mask_rows[:], 0.0)
         nc.sync.dma_start(
             out=mask_rows[0 : B * FT, :], in_=mask.rearrange("b o (f t) -> (b o f) t", t=P)
         )
+        load_w(0)
+        load_h(0)
+        load_w(1)
+        load_w(2)
+        load_h(1)
+        load_x(0)
+        load_x(1)
+        load_h(2)
+        load_x(2)
+        load_h(3)
+        load_x(3)
         nc.scalar.dma_start(out=gain[:], in_=g2.rearrange("(s p j) -> p s j", s=2, j=CT))
         nc.scalar.dma_start(out=shift[:], in_=be2.rearrange("(s p j) -> p s j", s=2, j=CT))
-        for b in range(B):
-            nc.sync.dma_start(out=h_raw[:, b], in_=h_view[b])
-            if b == 0:
-                for part in range(LOAD_PARTS):
-                    ks = slice(part * per_part * H, (part + 1) * per_part * H)
-                    nc.sync.dma_start(out=w_raw[:, ks], in_=w_view[:, ks])
-            for part in range(LOAD_PARTS):
-                js = slice(part * per_part, (part + 1) * per_part)
-                nc.sync.dma_start(out=x_sb[:, b, js, :], in_=x_view[b][:, js, :])
 
         bias_rows = keep.tile([P, P], F32)
         nc.vector.tensor_scalar(
             out=bias_rows[:], in0=mask_rows[:], scalar1=-1.0, scalar2=MASKED, op0=ALU.add, op1=ALU.mult
         )
-        bias_turned = psum_small.tile([P, P], F32)
+        bias_turned = psum_t.tile([P, P], F32, tag="logits_t")
         nc.tensor.transpose(bias_turned[:], bias_rows[:], ident[:])
         mask_bias = keep.tile([P, B * FT], F32)
         nc.vector.tensor_copy(out=mask_bias[:], in_=bias_turned[:, 0 : B * FT])
@@ -97,6 +110,11 @@ def tile_attentivestatspool_pb_kernel(tc, h, x, mask, w2, b2, g2, be2, out):
         w_grouped = keep.tile([P, C * PACK], BF16, align_bytes=64)
         w_codes = keep.tile([P, C], U32, align_bytes=64)
         w_scales = keep.tile([P, C], U8, align_bytes=64)
+
+        def regroup_h_on_vector(b):
+            nc.vector.tensor_copy(
+                out=h_grouped[:, b], in_=h_raw[:, b].rearrange("p v t -> p t v")
+            )
 
         def regroup_h_part(b, part):
             ts = slice(part * (T // H_PARTS), (part + 1) * (T // H_PARTS))
@@ -113,16 +131,22 @@ def tile_attentivestatspool_pb_kernel(tc, h, x, mask, w2, b2, g2, be2, out):
 
         w_words = w_raw[:].bitcast(F32).rearrange("p (j q u) -> p j u q", j=CT, u=2)
         w_grouped_words = w_grouped[:].bitcast(F32).rearrange("p (j c u) -> p j c u", j=CT, u=2)
+        turned_of = {}
 
-        def prepare_w_pair(pair):
-            turned = psum_t.tile([P, 2, 2, P], F32, tag="logits_t")
+        def turn_w_pair(pair):
+            turned = psum_c.tile([P, 2, 2, P], F32, tag="logits_c")
             for jj in range(2):
                 for u in range(2):
                     nc.tensor.transpose(turned[:, jj, u, :], w_words[:, 2 * pair + jj, u, :], ident[:])
+            turned_of[pair] = turned
+
+        def copy_w_pair(pair):
             nc.scalar.copy(
                 out=w_grouped_words[:, 2 * pair : 2 * pair + 2, :, :],
-                in_=turned[:].rearrange("p j u c -> p j c u"),
+                in_=turned_of[pair][:].rearrange("p j u c -> p j c u"),
             )
+
+        def quantise_w_pair(pair):
             cs = slice(2 * pair * P, (2 * pair + 2) * P)
             nc.vector.quantize_mx(
                 out=w_codes[:, cs].bitcast(FP8X4),
@@ -130,62 +154,62 @@ def tile_attentivestatspool_pb_kernel(tc, h, x, mask, w2, b2, g2, be2, out):
                 in_=w_grouped[:, 2 * pair * P * PACK : (2 * pair + 2) * P * PACK],
             )
 
-        for part in range(H_PARTS):
-            regroup_h_part(0, part)
-        quantise_h(0)
-        for pair in range(W_PAIRS_AT_START):
-            prepare_w_pair(pair)
-
         neg_max = keep.tile([P, TILES], F32)
         sum_e = keep.tile([P, TILES], F32)
         sum_ex = keep.tile([P, TILES], F32)
         sum_exx = keep.tile([P, TILES], F32)
+        logits_t_of = {}
         masked_t_of = {}
         logits_of = {}
         e_of = {}
         ex_of = {}
-        exx_of = {}
 
-        def masked_logits_by_frame(n):
-            b, rest = divmod(n, CT)
-            g, f = divmod(rest, FT)
-            logits_t = psum_t.tile([P, WIDE], F32, tag="logits_t")
-            nc.tensor.matmul_mx(
-                out=logits_t[:],
-                lhsT=h_codes[:, b, f * P : (f + 1) * P].bitcast(FP8X4),
-                lhsT_scale=h_scales[:, b, f * P : (f + 1) * P],
-                rhs=w_codes[:, g * WIDE : (g + 1) * WIDE].bitcast(FP8X4),
-                rhs_scale=w_scales[:, g * WIDE : (g + 1) * WIDE],
-                start=True,
-                stop=True,
-            )
-            if f == 0:
-                masked_t = work.tile([P, FT, WIDE], F32)
-                masked_t_of[n // FT] = masked_t
-            nc.scalar.activation(
-                out=masked_t_of[n // FT][:, f, :],
-                in_=logits_t[:],
-                func=ACT.Identity,
-                bias=mask_bias[:, b * FT + f : b * FT + f + 1],
-                scale=1.0,
-            )
-
-        def turn_back(i):
-            group, jj = divmod(i, GROUP)
-            logits = psum_c.tile([P, T], F32)
+        def multiply(g):
+            b, cg = divmod(g, GROUPS_PER_B)
             for f in range(FT):
-                nc.tensor.transpose(
-                    logits[:, f * P : (f + 1) * P],
-                    masked_t_of[group][:, f, jj * P : (jj + 1) * P],
-                    ident[:],
+                logits_t = psum_t.tile([P, WIDE], F32, tag="logits_t")
+                nc.tensor.matmul_mx(
+                    out=logits_t[:],
+                    lhsT=h_codes[:, b, f * P : (f + 1) * P].bitcast(FP8X4),
+                    lhsT_scale=h_scales[:, b, f * P : (f + 1) * P],
+                    rhs=w_codes[:, cg * WIDE : (cg + 1) * WIDE].bitcast(FP8X4),
+                    rhs_scale=w_scales[:, cg * WIDE : (cg + 1) * WIDE],
+                    start=True,
+                    stop=True,
                 )
-            logits_of[i] = logits
+                logits_t_of[(g, f)] = logits_t
 
-        def exponentials(i):
+        def mask_out(g):
+            b = g // GROUPS_PER_B
+            masked_t = masked_pool.tile([P, FT, WIDE], F32)
+            masked_t_of[g] = masked_t
+            for f in range(FT):
+                nc.scalar.activation(
+                    out=masked_t[:, f, :],
+                    in_=logits_t_of[(g, f)][:],
+                    func=ACT.Identity,
+                    bias=mask_bias[:, b * FT + f : b * FT + f + 1],
+                    scale=1.0,
+                )
+
+        def turn_back(g):
+            for jj in range(GROUP):
+                logits = psum_c.tile([P, T], F32, tag="logits_c")
+                for f in range(FT):
+                    nc.tensor.transpose(
+                        logits[:, f * P : (f + 1) * P],
+                        masked_t_of[g][:, f, jj * P : (jj + 1) * P],
+                        ident[:],
+                    )
+                logits_of[g * GROUP + jj] = logits
+
+        def maximum(i):
             nc.vector.tensor_reduce(
                 out=neg_max[:, i : i + 1], in_=logits_of[i][:], axis=AXIS.X, op=ALU.max, negate=True
             )
-            e = work.tile([P, T], F32)
+
+        def exponentials(i):
+            e = e_pool.tile([P, T], F32)
             nc.scalar.activation(
                 out=e[:],
                 in_=logits_of[i][:],
@@ -198,7 +222,7 @@ def tile_attentivestatspool_pb_kernel(tc, h, x, mask, w2, b2, g2, be2, out):
 
         def first_moment(i):
             b, j = divmod(i, CT)
-            ex = work.tile([P, T], F32)
+            ex = ex_pool.tile([P, T], F32)
             nc.vector.scalar_tensor_tensor(
                 out=ex[:],
                 in0=e_of[i][:],
@@ -212,40 +236,73 @@ def tile_attentivestatspool_pb_kernel(tc, h, x, mask, w2, b2, g2, be2, out):
 
         def second_moment(i):
             b, j = divmod(i, CT)
-            exx = work.tile([P, T], F32)
-            nc.vector.tensor_tensor(out=exx[:], in0=ex_of[i][:], in1=x_sb[:, b, j, :], op=ALU.mult)
-            exx_of[i] = exx
-
-        def sum_second_moment(i):
-            nc.scalar.activation(
-                out=exx_of[i][:], in_=exx_of[i][:], func=ACT.Copy, accum_out=sum_exx[:, i : i + 1]
+            exx = junk_pool.tile([P, T], F32)
+            nc.vector.scalar_tensor_tensor(
+                out=exx[:],
+                in0=ex_of[i][:],
+                scalar=1.0,
+                in1=x_sb[:, b, j, :],
+                op0=ALU.mult,
+                op1=ALU.mult,
+                accum_out=sum_exx[:, i : i + 1],
             )
 
-        def prepare_ahead(n):
-            if W_PAIRS_AT_START + n < W_PAIRS:
-                prepare_w_pair(W_PAIRS_AT_START + n)
-            b, rest = divmod(n, CT)
-            if b + 1 < B:
-                if H_FIRST_ROUND <= rest < H_FIRST_ROUND + H_PARTS:
-                    regroup_h_part(b + 1, rest - H_FIRST_ROUND)
-                if rest == H_FIRST_ROUND + H_PARTS + 1:
-                    quantise_h(b + 1)
+        turn_w_pair(0)
+        turn_w_pair(1)
+        copy_w_pair(0)
+        copy_w_pair(1)
+        regroup_h_on_vector(0)
+        quantise_w_pair(0)
+        quantise_w_pair(1)
+        quantise_h(0)
+        turn_w_pair(2)
+        turn_w_pair(3)
+        copy_w_pair(2)
+        copy_w_pair(3)
+        multiply(0)
+        mask_out(0)
+        turn_w_pair(4)
+        turn_w_pair(5)
+        quantise_w_pair(2)
+        quantise_w_pair(3)
+        regroup_h_on_vector(1)
+        quantise_h(1)
+        copy_w_pair(4)
+        copy_w_pair(5)
+        turn_back(0)
+        multiply(1)
 
-        for n in range(TILES + SUM_LAG + 1):
-            if n < TILES:
-                masked_logits_by_frame(n)
-            if TURN_LAG <= n < TILES + TURN_LAG:
-                turn_back(n - TURN_LAG)
-            if SUM_LAG <= n < TILES + SUM_LAG:
-                first_moment(n - SUM_LAG)
-            if EXP_LAG <= n < TILES + EXP_LAG:
-                exponentials(n - EXP_LAG)
-            if SUM_LAG <= n < TILES + SUM_LAG:
-                second_moment(n - SUM_LAG)
-            if n > SUM_LAG:
-                sum_second_moment(n - SUM_LAG - 1)
-            if n < TILES:
-                prepare_ahead(n)
+        for r in range(GROUPS):
+            first = r * GROUP
+            for k in range(GROUP):
+                maximum(first + k)
+                exponentials(first + k)
+            if r == 0:
+                quantise_w_pair(4)
+                quantise_w_pair(5)
+                mask_out(1)
+            if r % GROUPS_PER_B == 0 and 0 < r < GROUPS - GROUPS_PER_B:
+                quantise_h(r // GROUPS_PER_B + 1)
+            if r + 1 < GROUPS:
+                turn_back(r + 1)
+            if r == 0:
+                multiply(2)
+            if r + 2 < GROUPS:
+                mask_out(r + 2)
+            if r + 3 < GROUPS:
+                multiply(r + 3)
+            first_moment(first)
+            first_moment(first + 1)
+            second_moment(first)
+            first_moment(first + 2)
+            second_moment(first + 1)
+            first_moment(first + 3)
+            second_moment(first + 2)
+            second_moment(first + 3)
+            b_ahead, phase = divmod(r, GROUPS_PER_B)
+            if phase > 0 and b_ahead + 2 < B:
+                regroup_h_part(b_ahead + 2, 2 * (phase - 1))
+                regroup_h_part(b_ahead + 2, 2 * (phase - 1) + 1)
 
         nc.scalar.activation(out=warm_out[:], in_=warm_in[:], func=ACT.Sqrt)
 
@@ -272,7 +329,7 @@ def tile_attentivestatspool_pb_kernel(tc, h, x, mask, w2, b2, g2, be2, out):
         def total_over_all(values, name):
             row = keep.tile([P, B], F32, name="row_" + name)
             nc.vector.tensor_reduce(out=row[:], in_=values, axis=AXIS.X, op=ALU.add)
-            total = psum_small.tile([P, B], F32, name="total_" + name)
+            total = psum_t.tile([P, B], F32, name="total_" + name, tag="logits_t")
             nc.tensor.matmul(out=total[:], lhsT=ones[:], rhs=row[:], start=True, stop=True)
             return total
 

@@ -39,8 +39,9 @@ def tile_attentivestatspool_pb_kernel(tc, h, x, mask, w2, b2, g2, be2, out):
         keep = ctx.enter_context(tc.tile_pool(name="keep", bufs=1))
         masked_pool = ctx.enter_context(tc.tile_pool(name="masked_pool", bufs=3))
         e_pool = ctx.enter_context(tc.tile_pool(name="e_pool", bufs=6))
-        ex_pool = ctx.enter_context(tc.tile_pool(name="ex_pool", bufs=3))
+        ex_pool = ctx.enter_context(tc.tile_pool(name="ex_pool", bufs=8))
         junk_pool = ctx.enter_context(tc.tile_pool(name="junk_pool", bufs=2))
+        exx_pool = ctx.enter_context(tc.tile_pool(name="exx_pool", bufs=4))
         psum_t = ctx.enter_context(tc.psum_pool(name="psum_t", bufs=4))
         psum_c = ctx.enter_context(tc.psum_pool(name="psum_c", bufs=4))
 
@@ -163,6 +164,7 @@ def tile_attentivestatspool_pb_kernel(tc, h, x, mask, w2, b2, g2, be2, out):
         logits_of = {}
         e_of = {}
         ex_of = {}
+        exx_of = {}
 
         def multiply(g):
             b, cg = divmod(g, GROUPS_PER_B)
@@ -247,6 +249,17 @@ def tile_attentivestatspool_pb_kernel(tc, h, x, mask, w2, b2, g2, be2, out):
                 accum_out=sum_exx[:, i : i + 1],
             )
 
+        def second_moment_on_gpsimd(i):
+            b, j = divmod(i, CT)
+            exx = exx_pool.tile([P, T], F32)
+            nc.gpsimd.tensor_tensor(out=exx[:], in0=ex_of[i][:], in1=x_sb[:, b, j, :], op=ALU.mult)
+            exx_of[i] = exx
+
+        def sum_second_moment(i):
+            nc.scalar.activation(
+                out=exx_of[i][:], in_=exx_of[i][:], func=ACT.Copy, accum_out=sum_exx[:, i : i + 1]
+            )
+
         turn_w_pair(0)
         turn_w_pair(1)
         copy_w_pair(0)
@@ -291,19 +304,23 @@ def tile_attentivestatspool_pb_kernel(tc, h, x, mask, w2, b2, g2, be2, out):
                 mask_out(r + 2)
             if r + 3 < GROUPS:
                 multiply(r + 3)
-            first_moment(first)
-            first_moment(first + 1)
-            second_moment(first)
-            first_moment(first + 2)
-            second_moment(first + 1)
-            first_moment(first + 3)
-            second_moment(first + 2)
-            second_moment(first + 3)
+            if r > 0:
+                sum_second_moment(first - 1)
+                sum_second_moment(first - 2)
+                second_moment(first - GROUP)
+                second_moment(first - GROUP + 1)
+            for k in range(GROUP):
+                first_moment(first + k)
+            if r + 1 < GROUPS:
+                second_moment_on_gpsimd(first + 3)
+                second_moment_on_gpsimd(first + 2)
             b_ahead, phase = divmod(r, GROUPS_PER_B)
             if phase > 0 and b_ahead + 2 < B:
                 regroup_h_part(b_ahead + 2, 2 * (phase - 1))
                 regroup_h_part(b_ahead + 2, 2 * (phase - 1) + 1)
 
+        for k in range(GROUP):
+            second_moment(TILES - GROUP + k)
         nc.scalar.activation(out=warm_out[:], in_=warm_in[:], func=ACT.Sqrt)
 
         def by_utterance(t):

@@ -305,15 +305,15 @@ def tile_attentivestatspool_pb_kernel(tc, h, x, mask, w2, b2, g2, be2, out):
             if r + 3 < GROUPS:
                 multiply(r + 3)
             if r > 0:
-                sum_second_moment(first - 1)
                 sum_second_moment(first - 2)
+                sum_second_moment(first - 1)
                 second_moment(first - GROUP)
                 second_moment(first - GROUP + 1)
             for k in range(GROUP):
                 first_moment(first + k)
             if r + 1 < GROUPS:
-                second_moment_on_gpsimd(first + 3)
                 second_moment_on_gpsimd(first + 2)
+                second_moment_on_gpsimd(first + 3)
             b_ahead, phase = divmod(r, GROUPS_PER_B)
             if phase > 0 and b_ahead + 2 < B:
                 regroup_h_part(b_ahead + 2, 2 * (phase - 1))

@@ -66,8 +66,8 @@ def tile_attentivestatspool_pb_kernel(tc, h, x, mask, w2, b2, g2, be2, out):
         x_view = x.rearrange("b (p j) t -> b p j t", j=CT)
         per_part = CT // LOAD_PARTS
 
-        def load_w(part):
-            ks = slice(part * per_part * H, (part + 1) * per_part * H)
+        def load_w(first_tile, tiles):
+            ks = slice(first_tile * H, (first_tile + tiles) * H)
             nc.sync.dma_start(out=w_raw[:, ks], in_=w_view[:, ks])
 
         def load_h(b):
@@ -79,13 +79,14 @@ def tile_attentivestatspool_pb_kernel(tc, h, x, mask, w2, b2, g2, be2, out):
                 nc.sync.dma_start(out=x_sb[:, b, js, :], in_=x_view[b][:, js, :])
 
         nc.vector.memset(mask_rows[:], 0.0)
+        load_w(0, 2)
+        load_h(0)
+        load_w(2, 2)
         nc.sync.dma_start(
             out=mask_rows[0 : B * FT, :], in_=mask.rearrange("b o (f t) -> (b o f) t", t=P)
         )
-        load_w(0)
-        load_h(0)
-        load_w(1)
-        load_w(2)
+        load_w(4, 4)
+        load_w(8, 4)
         load_h(1)
         load_x(0)
         load_x(1)
@@ -97,13 +98,7 @@ def tile_attentivestatspool_pb_kernel(tc, h, x, mask, w2, b2, g2, be2, out):
         nc.scalar.dma_start(out=shift[:], in_=be2.rearrange("(s p j) -> p s j", s=2, j=CT))
 
         bias_rows = keep.tile([P, P], F32)
-        nc.vector.tensor_scalar(
-            out=bias_rows[:], in0=mask_rows[:], scalar1=-1.0, scalar2=MASKED, op0=ALU.add, op1=ALU.mult
-        )
-        bias_turned = psum_t.tile([P, P], F32, tag="logits_t")
-        nc.tensor.transpose(bias_turned[:], bias_rows[:], ident[:])
         mask_bias = keep.tile([P, B * FT], F32)
-        nc.vector.tensor_copy(out=mask_bias[:], in_=bias_turned[:, 0 : B * FT])
 
         h_grouped = keep.tile([P, B, T, PACK], BF16, align_bytes=64)
         h_codes = keep.tile([P, B, T], U32, align_bytes=64)
@@ -265,9 +260,15 @@ def tile_attentivestatspool_pb_kernel(tc, h, x, mask, w2, b2, g2, be2, out):
         copy_w_pair(0)
         copy_w_pair(1)
         regroup_h_on_vector(0)
+        nc.vector.tensor_scalar(
+            out=bias_rows[:], in0=mask_rows[:], scalar1=-1.0, scalar2=MASKED, op0=ALU.add, op1=ALU.mult
+        )
+        bias_turned = psum_t.tile([P, P], F32, tag="logits_t")
+        nc.tensor.transpose(bias_turned[:], bias_rows[:], ident[:])
         quantise_w_pair(0)
-        quantise_w_pair(1)
         quantise_h(0)
+        quantise_w_pair(1)
+        nc.vector.tensor_copy(out=mask_bias[:], in_=bias_turned[:, 0 : B * FT])
         turn_w_pair(2)
         turn_w_pair(3)
         copy_w_pair(2)
@@ -319,66 +320,67 @@ def tile_attentivestatspool_pb_kernel(tc, h, x, mask, w2, b2, g2, be2, out):
                 regroup_h_part(b_ahead + 2, 2 * (phase - 1))
                 regroup_h_part(b_ahead + 2, 2 * (phase - 1) + 1)
 
-        for k in range(GROUP):
-            second_moment(TILES - GROUP + k)
-        nc.scalar.activation(out=warm_out[:], in_=warm_in[:], func=ACT.Sqrt)
-
         def by_utterance(t):
             return t[:].rearrange("p (b j) -> p b j", b=B)
 
         stats = keep.tile([P, B, 2, CT], F32)
-        mean = stats[:, :, 0, :]
+        squares = keep.tile([P, B, 2, CT], F32)
         inv_e = keep.tile([P, TILES], F32)
-        second = keep.tile([P, B, CT], F32)
-        mean_sq = keep.tile([P, B, CT], F32)
+        second_moment(TILES - GROUP)
         nc.vector.reciprocal(out=inv_e[:], in_=sum_e[:])
-        nc.vector.tensor_mul(out=mean, in0=by_utterance(sum_ex), in1=by_utterance(inv_e))
-        nc.vector.tensor_mul(out=second[:], in0=by_utterance(sum_exx), in1=by_utterance(inv_e))
-        nc.vector.tensor_mul(out=mean_sq[:], in0=mean, in1=mean)
-        nc.vector.tensor_sub(out=second[:], in0=second[:], in1=mean_sq[:])
-        nc.vector.tensor_scalar_max(out=second[:], in0=second[:], scalar1=EPS_STD)
-        nc.scalar.activation(out=stats[:, :, 1, :], in_=second[:], func=ACT.Sqrt)
+        second_moment(TILES - GROUP + 1)
+        nc.vector.tensor_mul(out=stats[:, :, 0, :], in0=by_utterance(sum_ex), in1=by_utterance(inv_e))
+        second_moment(TILES - GROUP + 2)
+        nc.vector.tensor_mul(out=squares[:, :, 0, :], in0=stats[:, :, 0, :], in1=stats[:, :, 0, :])
+        second_moment(TILES - GROUP + 3)
+        nc.scalar.activation(out=warm_out[:], in_=warm_in[:], func=ACT.Sqrt)
 
         entries = 2 * C
         width = 2 * CT
+        rows = keep.tile([P, 2 * B], F32)
+        second = keep.tile([P, B, CT], F32)
         flat = stats[:].rearrange("p b s j -> p b (s j)")
 
-        def total_over_all(values, name):
-            row = keep.tile([P, B], F32, name="row_" + name)
-            nc.vector.tensor_reduce(out=row[:], in_=values, axis=AXIS.X, op=ALU.add)
-            total = psum_t.tile([P, B], F32, name="total_" + name, tag="logits_t")
-            nc.tensor.matmul(out=total[:], lhsT=ones[:], rhs=row[:], start=True, stop=True)
-            return total
-
         def along_entries(t):
-            return t[:].unsqueeze(2).to_broadcast([P, B, width])
+            return t.unsqueeze(2).to_broadcast([P, B, width])
 
         def along_utterances(t):
             return t[:].rearrange("p s j -> p (s j)").unsqueeze(1).to_broadcast([P, B, width])
 
-        mu = keep.tile([P, B], F32)
-        centred = keep.tile([P, B, width], F32)
-        squared = keep.tile([P, B, width], F32)
+        nc.vector.tensor_mul(out=second[:], in0=by_utterance(sum_exx), in1=by_utterance(inv_e))
+        nc.vector.tensor_sub(out=second[:], in0=second[:], in1=squares[:, :, 0, :])
+        nc.vector.tensor_scalar_max(out=squares[:, :, 1, :], in0=second[:], scalar1=EPS_STD)
+        nc.scalar.activation(out=stats[:, :, 1, :], in_=squares[:, :, 1, :], func=ACT.Sqrt)
+        nc.vector.tensor_reduce(
+            out=rows[:, B : 2 * B], in_=squares[:].rearrange("p b s j -> p b (s j)"), axis=AXIS.X, op=ALU.add
+        )
+        nc.vector.tensor_reduce(out=rows[:, 0:B], in_=flat, axis=AXIS.X, op=ALU.add)
+
+        totals = psum_t.tile([P, 2 * B], F32, tag="logits_t")
+        nc.tensor.matmul(out=totals[:], lhsT=ones[:], rhs=rows[:], start=True, stop=True)
+        scaled = keep.tile([P, B, width], F32)
+        nc.vector.tensor_mul(out=scaled[:], in0=flat, in1=along_utterances(gain))
+        neg_mu = keep.tile([P, B], F32)
         spread = keep.tile([P, B], F32)
-        nc.vector.tensor_scalar_mul(out=mu[:], in0=total_over_all(flat, "v")[:], scalar1=1.0 / entries)
-        nc.vector.tensor_sub(out=centred[:], in0=flat, in1=along_entries(mu))
-        nc.vector.tensor_mul(out=squared[:], in0=centred[:], in1=centred[:])
-        nc.vector.tensor_scalar(
+        centred = keep.tile([P, B, width], F32)
+        nc.vector.tensor_scalar_mul(out=neg_mu[:], in0=totals[:, 0:B], scalar1=-1.0 / entries)
+        nc.vector.tensor_mul(out=spread[:], in0=neg_mu[:], in1=totals[:, 0:B])
+        nc.vector.scalar_tensor_tensor(
             out=spread[:],
-            in0=total_over_all(squared[:], "sq")[:],
-            scalar1=1.0 / entries,
-            scalar2=EPS_LN,
-            op0=ALU.mult,
+            in0=spread[:],
+            scalar=entries * EPS_LN,
+            in1=totals[:, B : 2 * B],
+            op0=ALU.add,
             op1=ALU.add,
         )
-        nc.scalar.activation(out=spread[:], in_=spread[:], func=ACT.Sqrt)
+        nc.scalar.activation(out=spread[:], in_=spread[:], func=ACT.Sqrt, scale=1.0 / entries)
+        nc.vector.tensor_mul(out=centred[:], in0=along_utterances(gain), in1=along_entries(neg_mu[:]))
+        nc.vector.tensor_add(out=centred[:], in0=centred[:], in1=scaled[:])
         nc.vector.reciprocal(out=spread[:], in_=spread[:])
-        nc.vector.tensor_mul(out=centred[:], in0=centred[:], in1=along_entries(spread))
-        nc.vector.tensor_mul(out=centred[:], in0=centred[:], in1=along_utterances(gain))
+        nc.vector.tensor_mul(out=centred[:], in0=centred[:], in1=along_entries(spread[:]))
         nc.vector.tensor_add(out=centred[:], in0=centred[:], in1=along_utterances(shift))
 
-        out_view = out.rearrange("b (s p j) o -> b p s (j o)", s=2, j=CT)
-        for b in range(B):
-            nc.sync.dma_start(
-                out=out_view[b], in_=centred[:, b, :].rearrange("p (s j) -> p s j", s=2)
-            )
+        nc.sync.dma_start(
+            out=out.rearrange("b (s p j) o -> p (b s) (j o)", s=2, j=CT),
+            in_=centred[:].rearrange("p b (s j) -> p (b s) j", s=2),
+        )

@@ -23,7 +23,6 @@ TILES = B * CT
 GROUPS = TILES // GROUP
 GROUPS_PER_B = CT // GROUP
 W_PAIRS = CT // 2
-H_PARTS = 4
 LOAD_PARTS = 3
 EPS_STD = 1e-5
 EPS_LN = 1e-5
@@ -110,12 +109,6 @@ def tile_attentivestatspool_pb_kernel(tc, h, x, mask, w2, b2, g2, be2, out):
         def regroup_h_on_vector(b):
             nc.vector.tensor_copy(
                 out=h_grouped[:, b], in_=h_raw[:, b].rearrange("p v t -> p t v")
-            )
-
-        def regroup_h_part(b, part):
-            ts = slice(part * (T // H_PARTS), (part + 1) * (T // H_PARTS))
-            nc.scalar.copy(
-                out=h_grouped[:, b, ts, :], in_=h_raw[:, b, :, ts].rearrange("p v t -> p t v")
             )
 
         def quantise_h(b):
@@ -310,15 +303,13 @@ def tile_attentivestatspool_pb_kernel(tc, h, x, mask, w2, b2, g2, be2, out):
                 sum_second_moment(first - 1)
                 second_moment(first - GROUP)
                 second_moment(first - GROUP + 1)
+            if r % GROUPS_PER_B == 1 and r // GROUPS_PER_B + 2 < B:
+                regroup_h_on_vector(r // GROUPS_PER_B + 2)
             for k in range(GROUP):
                 first_moment(first + k)
             if r + 1 < GROUPS:
                 second_moment_on_gpsimd(first + 2)
                 second_moment_on_gpsimd(first + 3)
-            b_ahead, phase = divmod(r, GROUPS_PER_B)
-            if phase > 0 and b_ahead + 2 < B:
-                regroup_h_part(b_ahead + 2, 2 * (phase - 1))
-                regroup_h_part(b_ahead + 2, 2 * (phase - 1) + 1)
 
         def by_utterance(t):
             return t[:].rearrange("p (b j) -> p b j", b=B)

@@ -46,6 +46,8 @@ def tile_attentivestatspool_pb_kernel(tc, h, x, mask, w2, b2, g2, be2, out):
 
         ident = keep.tile([P, P], F32)
         make_identity(nc, ident[:])
+        ident_bf16 = keep.tile([P, P], BF16)
+        nc.vector.tensor_copy(out=ident_bf16[:], in_=ident[:])
         ones = keep.tile([P, P], F32)
         nc.vector.memset(ones[:], 1.0)
         warm_in = keep.tile([P, 1], F32)
@@ -153,6 +155,7 @@ def tile_attentivestatspool_pb_kernel(tc, h, x, mask, w2, b2, g2, be2, out):
         e_of = {}
         ex_of = {}
         exx_of = {}
+        x_of = {}
 
         def multiply(g):
             b, cg = divmod(g, GROUPS_PER_B)
@@ -193,6 +196,19 @@ def tile_attentivestatspool_pb_kernel(tc, h, x, mask, w2, b2, g2, be2, out):
                     )
                 logits_of[g * GROUP + jj] = logits
 
+        def copy_x_to_psum(g):
+            for i in range(g * GROUP, (g + 1) * GROUP):
+                b, j = divmod(i, CT)
+                bank = psum_t.tile([P, T], BF16, tag="logits_t")
+                nc.tensor.matmul(
+                    out=bank[:], lhsT=ident_bf16[:], rhs=x_sb[:, b, j, :], start=True, stop=True
+                )
+                x_of[i] = bank[:]
+
+        def x_for_vector(i):
+            b, j = divmod(i, CT)
+            return x_of.get(i, x_sb[:, b, j, :])
+
         def maximum(i):
             nc.vector.tensor_reduce(
                 out=neg_max[:, i : i + 1], in_=logits_of[i][:], axis=AXIS.X, op=ALU.max, negate=True
@@ -211,13 +227,12 @@ def tile_attentivestatspool_pb_kernel(tc, h, x, mask, w2, b2, g2, be2, out):
             e_of[i] = e
 
         def first_moment(i):
-            b, j = divmod(i, CT)
             ex = ex_pool.tile([P, T], F32)
             nc.vector.scalar_tensor_tensor(
                 out=ex[:],
                 in0=e_of[i][:],
                 scalar=1.0,
-                in1=x_sb[:, b, j, :],
+                in1=x_for_vector(i),
                 op0=ALU.mult,
                 op1=ALU.mult,
                 accum_out=sum_ex[:, i : i + 1],
@@ -225,13 +240,12 @@ def tile_attentivestatspool_pb_kernel(tc, h, x, mask, w2, b2, g2, be2, out):
             ex_of[i] = ex
 
         def second_moment(i):
-            b, j = divmod(i, CT)
             exx = junk_pool.tile([P, T], F32)
             nc.vector.scalar_tensor_tensor(
                 out=exx[:],
                 in0=ex_of[i][:],
                 scalar=1.0,
-                in1=x_sb[:, b, j, :],
+                in1=x_for_vector(i),
                 op0=ALU.mult,
                 op1=ALU.mult,
                 accum_out=sum_exx[:, i : i + 1],
@@ -279,6 +293,14 @@ def tile_attentivestatspool_pb_kernel(tc, h, x, mask, w2, b2, g2, be2, out):
         turn_back(0)
         multiply(1)
 
+        def on_gpsimd(g):
+            first = g * GROUP
+            if g == GROUPS - 1:
+                return (first,)
+            if g >= GROUPS - 3:
+                return (first + 2, first + 3, first, first + 1)
+            return (first + 2, first + 3)
+
         for r in range(GROUPS):
             first = r * GROUP
             for k in range(GROUP):
@@ -299,17 +321,19 @@ def tile_attentivestatspool_pb_kernel(tc, h, x, mask, w2, b2, g2, be2, out):
             if r + 3 < GROUPS:
                 multiply(r + 3)
             if r > 0:
-                sum_second_moment(first - 2)
-                sum_second_moment(first - 1)
-                second_moment(first - GROUP)
-                second_moment(first - GROUP + 1)
+                for i in on_gpsimd(r - 1):
+                    sum_second_moment(i)
+                for k in range(GROUP):
+                    if first - GROUP + k not in on_gpsimd(r - 1):
+                        second_moment(first - GROUP + k)
+            if GROUPS - 3 <= r < GROUPS - 1:
+                copy_x_to_psum(r + 1)
             if r % GROUPS_PER_B == 1 and r // GROUPS_PER_B + 2 < B:
                 regroup_h_on_vector(r // GROUPS_PER_B + 2)
             for k in range(GROUP):
                 first_moment(first + k)
-            if r + 1 < GROUPS:
-                second_moment_on_gpsimd(first + 2)
-                second_moment_on_gpsimd(first + 3)
+            for i in on_gpsimd(r):
+                second_moment_on_gpsimd(i)
 
         def by_utterance(t):
             return t[:].rearrange("p (b j) -> p b j", b=B)
@@ -317,9 +341,9 @@ def tile_attentivestatspool_pb_kernel(tc, h, x, mask, w2, b2, g2, be2, out):
         stats = keep.tile([P, B, 2, CT], F32)
         squares = keep.tile([P, B, 2, CT], F32)
         inv_e = keep.tile([P, TILES], F32)
-        second_moment(TILES - GROUP)
-        nc.vector.reciprocal(out=inv_e[:], in_=sum_e[:])
+        sum_second_moment(TILES - GROUP)
         second_moment(TILES - GROUP + 1)
+        nc.vector.reciprocal(out=inv_e[:], in_=sum_e[:])
         nc.vector.tensor_mul(out=stats[:, :, 0, :], in0=by_utterance(sum_ex), in1=by_utterance(inv_e))
         second_moment(TILES - GROUP + 2)
         nc.vector.tensor_mul(out=squares[:, :, 0, :], in0=stats[:, :, 0, :], in1=stats[:, :, 0, :])

@@ -48,6 +48,9 @@ def tile_attentivestatspool_pb_kernel(tc, h, x, mask, w2, b2, g2, be2, out):
         make_identity(nc, ident[:])
         ident_bf16 = keep.tile([P, P], BF16)
         nc.vector.tensor_copy(out=ident_bf16[:], in_=ident[:])
+        evens_odds = keep.tile([P, 3, P // 2], F32)
+        for part in range(3):
+            nc.vector.tensor_copy(out=evens_odds[:, part, :], in_=ident[:, part % 2 : P : 2])
         ones = keep.tile([P, P], F32)
         nc.vector.memset(ones[:], 1.0)
         warm_in = keep.tile([P, 1], F32)
@@ -59,8 +62,8 @@ def tile_attentivestatspool_pb_kernel(tc, h, x, mask, w2, b2, g2, be2, out):
         h_raw = keep.tile([P, B, PACK, T], BF16)
         w_raw = keep.tile([P, CT * H], BF16)
         x_sb = keep.tile([P, B, CT, T], BF16)
-        gain = keep.tile([P, 2, CT], BF16)
-        shift = keep.tile([P, 2, CT], BF16)
+        gain = keep.tile([P // 2, 2, 2 * CT], BF16)
+        shift = keep.tile([P // 2, 2, 2 * CT], BF16)
 
         h_view = h.rearrange("b (p v) t -> b p v t", v=PACK)
         w_view = w2.rearrange("(p j) k -> p (j k)", j=CT)
@@ -95,8 +98,8 @@ def tile_attentivestatspool_pb_kernel(tc, h, x, mask, w2, b2, g2, be2, out):
         load_x(2)
         load_h(3)
         load_x(3)
-        nc.scalar.dma_start(out=gain[:], in_=g2.rearrange("(s p j) -> p s j", s=2, j=CT))
-        nc.scalar.dma_start(out=shift[:], in_=be2.rearrange("(s p j) -> p s j", s=2, j=CT))
+        nc.scalar.dma_start(out=gain[:], in_=g2.rearrange("(s m q) -> m s q", s=2, q=2 * CT))
+        nc.scalar.dma_start(out=shift[:], in_=be2.rearrange("(s m q) -> m s q", s=2, q=2 * CT))
 
         bias_rows = keep.tile([P, P], F32)
         mask_bias = keep.tile([P, B * FT], F32)
@@ -356,11 +359,14 @@ def tile_attentivestatspool_pb_kernel(tc, h, x, mask, w2, b2, g2, be2, out):
         second = keep.tile([P, B, CT], F32)
         flat = stats[:].rearrange("p b s j -> p b (s j)")
 
+        half = P // 2
+        pair_width = 2 * width
+
         def along_entries(t):
-            return t.unsqueeze(2).to_broadcast([P, B, width])
+            return t.unsqueeze(2).to_broadcast([half, B, pair_width])
 
         def along_utterances(t):
-            return t[:].rearrange("p s j -> p (s j)").unsqueeze(1).to_broadcast([P, B, width])
+            return t[:].rearrange("m s q -> m (s q)").unsqueeze(1).to_broadcast([half, B, pair_width])
 
         nc.vector.tensor_mul(out=second[:], in0=by_utterance(sum_exx), in1=by_utterance(inv_e))
         nc.vector.tensor_sub(out=second[:], in0=second[:], in1=squares[:, :, 0, :])
@@ -373,11 +379,20 @@ def tile_attentivestatspool_pb_kernel(tc, h, x, mask, w2, b2, g2, be2, out):
 
         totals = psum_t.tile([P, 2 * B], F32, tag="logits_t")
         nc.tensor.matmul(out=totals[:], lhsT=ones[:], rhs=rows[:], start=True, stop=True)
-        scaled = keep.tile([P, B, width], F32)
-        nc.vector.tensor_mul(out=scaled[:], in0=flat, in1=along_utterances(gain))
-        neg_mu = keep.tile([P, B], F32)
-        spread = keep.tile([P, B], F32)
-        centred = keep.tile([P, B, width], F32)
+        merged = psum_t.tile([P, 2 * B, 2, CT], F32, tag="logits_t")
+        for r in range(2):
+            nc.tensor.matmul(
+                out=merged[:, :, r, :],
+                lhsT=evens_odds[:].rearrange("p a m -> p (a m)")[:, r * half : r * half + P],
+                rhs=stats[:].rearrange("p b s j -> p (b s j)"),
+                start=True,
+                stop=True,
+            )
+        scaled = keep.tile([half, B, pair_width], F32)
+        neg_mu = keep.tile([half, B], F32)
+        spread = keep.tile([half, B], F32)
+        centred = keep.tile([half, B, pair_width], F32)
+        totals = totals[0:half, :]
         nc.vector.tensor_scalar_mul(out=neg_mu[:], in0=totals[:, 0:B], scalar1=-1.0 / entries)
         nc.vector.tensor_mul(out=spread[:], in0=neg_mu[:], in1=totals[:, 0:B])
         nc.vector.scalar_tensor_tensor(
@@ -390,12 +405,17 @@ def tile_attentivestatspool_pb_kernel(tc, h, x, mask, w2, b2, g2, be2, out):
         )
         nc.scalar.activation(out=spread[:], in_=spread[:], func=ACT.Sqrt, scale=1.0 / entries)
         nc.vector.tensor_mul(out=centred[:], in0=along_utterances(gain), in1=along_entries(neg_mu[:]))
+        nc.vector.tensor_mul(
+            out=scaled[:],
+            in0=merged[0:half, :, :, :].rearrange("m (b s) r j -> m b (s r j)", b=B),
+            in1=along_utterances(gain),
+        )
         nc.vector.tensor_add(out=centred[:], in0=centred[:], in1=scaled[:])
         nc.vector.reciprocal(out=spread[:], in_=spread[:])
         nc.vector.tensor_mul(out=centred[:], in0=centred[:], in1=along_entries(spread[:]))
         nc.vector.tensor_add(out=centred[:], in0=centred[:], in1=along_utterances(shift))
 
         nc.sync.dma_start(
-            out=out.rearrange("b (s p j) o -> p (b s) (j o)", s=2, j=CT),
-            in_=centred[:].rearrange("p b (s j) -> p (b s) j", s=2),
+            out=out.rearrange("b (s m q) o -> m (b s) (q o)", s=2, q=2 * CT),
+            in_=centred[:].rearrange("m b (s q) -> m (b s) q", s=2),
         )

@@ -74,8 +74,8 @@ def tile_attentivestatspool_pb_kernel(tc, h, x, mask, w2, b2, g2, be2, out):
             ks = slice(first_tile * H, (first_tile + tiles) * H)
             nc.sync.dma_start(out=w_raw[:, ks], in_=w_view[:, ks])
 
-        def load_h(b):
-            nc.sync.dma_start(out=h_raw[:, b], in_=h_view[b])
+        def load_h(b, ts=slice(0, T)):
+            nc.sync.dma_start(out=h_raw[:, b, :, ts], in_=h_view[b][:, :, ts])
 
         def load_x(b):
             for part in range(LOAD_PARTS):
@@ -83,20 +83,23 @@ def tile_attentivestatspool_pb_kernel(tc, h, x, mask, w2, b2, g2, be2, out):
                 nc.sync.dma_start(out=x_sb[:, b, js, :], in_=x_view[b][:, js, :])
 
         nc.vector.memset(mask_rows[:], 0.0)
+        first_half, second_half = slice(0, T // 2), slice(T // 2, T)
+        load_h(0, first_half)
         load_w(0, 2)
-        load_h(0)
+        load_h(0, second_half)
         load_w(2, 2)
         nc.sync.dma_start(
             out=mask_rows[0 : B * FT, :], in_=mask.rearrange("b o (f t) -> (b o f) t", t=P)
         )
-        load_w(4, 4)
-        load_w(8, 4)
+        load_w(4, 2)
         load_h(1)
+        load_w(6, 2)
+        load_w(8, 4)
         load_x(0)
-        load_x(1)
         load_h(2)
-        load_x(2)
         load_h(3)
+        load_x(1)
+        load_x(2)
         load_x(3)
         nc.scalar.dma_start(out=gain[:], in_=g2.rearrange("(s m q) -> m s q", s=2, q=2 * CT))
         nc.scalar.dma_start(out=shift[:], in_=be2.rearrange("(s m q) -> m s q", s=2, q=2 * CT))
@@ -111,16 +114,21 @@ def tile_attentivestatspool_pb_kernel(tc, h, x, mask, w2, b2, g2, be2, out):
         w_codes = keep.tile([P, C], U32, align_bytes=64)
         w_scales = keep.tile([P, C], U8, align_bytes=64)
 
-        def regroup_h_on_vector(b):
+        def regroup_h_on_vector(b, ts=slice(0, T)):
             nc.vector.tensor_copy(
-                out=h_grouped[:, b], in_=h_raw[:, b].rearrange("p v t -> p t v")
+                out=h_grouped[:, b, ts, :], in_=h_raw[:, b, :, ts].rearrange("p v t -> p t v")
             )
 
-        def quantise_h(b):
+        def regroup_h_on_scalar(b, ts=slice(0, T)):
+            nc.scalar.copy(
+                out=h_grouped[:, b, ts, :], in_=h_raw[:, b, :, ts].rearrange("p v t -> p t v")
+            )
+
+        def quantise_h(b, ts=slice(0, T)):
             nc.vector.quantize_mx(
-                out=h_codes[:, b, :].bitcast(FP8X4),
-                scales=h_scales[:, b, :],
-                in_=h_grouped[:, b].rearrange("p t v -> p (t v)"),
+                out=h_codes[:, b, ts].bitcast(FP8X4),
+                scales=h_scales[:, b, ts],
+                in_=h_grouped[:, b, ts, :].rearrange("p t v -> p (t v)"),
             )
 
         w_words = w_raw[:].bitcast(F32).rearrange("p (j q u) -> p j u q", j=CT, u=2)
@@ -134,8 +142,9 @@ def tile_attentivestatspool_pb_kernel(tc, h, x, mask, w2, b2, g2, be2, out):
                     nc.tensor.transpose(turned[:, jj, u, :], w_words[:, 2 * pair + jj, u, :], ident[:])
             turned_of[pair] = turned
 
-        def copy_w_pair(pair):
-            nc.scalar.copy(
+        def copy_w_pair(pair, on_vector=False):
+            copy = nc.vector.tensor_copy if on_vector else nc.scalar.copy
+            copy(
                 out=w_grouped_words[:, 2 * pair : 2 * pair + 2, :, :],
                 in_=turned_of[pair][:].rearrange("p j u c -> p j c u"),
             )
@@ -188,8 +197,38 @@ def tile_attentivestatspool_pb_kernel(tc, h, x, mask, w2, b2, g2, be2, out):
                     scale=1.0,
                 )
 
-        def turn_back(g):
-            for jj in range(GROUP):
+        def multiply_pair(pair):
+            cs = slice(2 * pair * P, (2 * pair + 2) * P)
+            for half in range(2):
+                bank = psum_t.tile([P, 2, 2 * P], F32, tag="logits_t")
+                for s in range(2):
+                    fs = slice((2 * half + s) * P, (2 * half + s + 1) * P)
+                    nc.tensor.matmul_mx(
+                        out=bank[:, s, :],
+                        lhsT=h_codes[:, 0, fs].bitcast(FP8X4),
+                        lhsT_scale=h_scales[:, 0, fs],
+                        rhs=w_codes[:, cs].bitcast(FP8X4),
+                        rhs_scale=w_scales[:, cs],
+                        start=True,
+                        stop=True,
+                    )
+                logits_t_of[(pair, half)] = bank
+
+        def mask_out_pair(pair):
+            if pair == 0:
+                masked_t = masked_pool.tile([P, FT, WIDE], F32)
+                masked_t_of[0] = masked_t
+            for f in range(FT):
+                nc.scalar.activation(
+                    out=masked_t_of[0][:, f, 2 * pair * P : (2 * pair + 2) * P],
+                    in_=logits_t_of[(pair, f // 2)][:, f % 2, :],
+                    func=ACT.Identity,
+                    bias=mask_bias[:, f : f + 1],
+                    scale=1.0,
+                )
+
+        def turn_back(g, tiles=range(GROUP)):
+            for jj in tiles:
                 logits = psum_c.tile([P, T], F32, tag="logits_c")
                 for f in range(FT):
                     nc.tensor.transpose(
@@ -269,32 +308,29 @@ def tile_attentivestatspool_pb_kernel(tc, h, x, mask, w2, b2, g2, be2, out):
         turn_w_pair(1)
         copy_w_pair(0)
         copy_w_pair(1)
-        regroup_h_on_vector(0)
+        regroup_h_on_vector(0, first_half)
+        quantise_h(0, first_half)
+        regroup_h_on_vector(0, second_half)
         nc.vector.tensor_scalar(
             out=bias_rows[:], in0=mask_rows[:], scalar1=-1.0, scalar2=MASKED, op0=ALU.add, op1=ALU.mult
         )
+        quantise_w_pair(0)
+        quantise_h(0, second_half)
         bias_turned = psum_t.tile([P, P], F32, tag="logits_t")
         nc.tensor.transpose(bias_turned[:], bias_rows[:], ident[:])
-        quantise_w_pair(0)
-        quantise_h(0)
-        quantise_w_pair(1)
         nc.vector.tensor_copy(out=mask_bias[:], in_=bias_turned[:, 0 : B * FT])
+        quantise_w_pair(1)
         turn_w_pair(2)
-        turn_w_pair(3)
         copy_w_pair(2)
-        copy_w_pair(3)
-        multiply(0)
-        mask_out(0)
-        turn_w_pair(4)
-        turn_w_pair(5)
-        quantise_w_pair(2)
-        quantise_w_pair(3)
+        multiply_pair(0)
+        mask_out_pair(0)
+        multiply_pair(1)
+        mask_out_pair(1)
+        turn_back(0)
+        turn_w_pair(3)
         regroup_h_on_vector(1)
         quantise_h(1)
-        copy_w_pair(4)
-        copy_w_pair(5)
-        turn_back(0)
-        multiply(1)
+        quantise_w_pair(2)
 
         def on_gpsimd(g):
             first = g * GROUP
@@ -310,33 +346,52 @@ def tile_attentivestatspool_pb_kernel(tc, h, x, mask, w2, b2, g2, be2, out):
                 maximum(first + k)
                 exponentials(first + k)
             if r == 0:
+                copy_w_pair(3, on_vector=True)
+                quantise_w_pair(3)
+                multiply(1)
+                mask_out(1)
+                turn_w_pair(4)
+                turn_w_pair(5)
+                turn_back(1)
+                copy_w_pair(4)
+                copy_w_pair(5)
+                first_moment(0)
+                first_moment(1)
+                regroup_h_on_vector(2)
+                second_moment(0)
+                second_moment(1)
                 quantise_w_pair(4)
                 quantise_w_pair(5)
-                mask_out(1)
-            if r % GROUPS_PER_B == 0 and 0 < r < GROUPS - GROUPS_PER_B:
-                quantise_h(r // GROUPS_PER_B + 1)
-            if r + 1 < GROUPS:
-                turn_back(r + 1)
-            if r == 0:
+                first_moment(2)
+                first_moment(3)
+                second_moment_on_gpsimd(2)
+                second_moment_on_gpsimd(3)
+                pass
                 multiply(2)
-            if r + 2 < GROUPS:
-                mask_out(r + 2)
-            if r + 3 < GROUPS:
-                multiply(r + 3)
-            if r > 0:
+                mask_out(2)
+                multiply(3)
+            else:
+                if r % GROUPS_PER_B == 0 and r < GROUPS - GROUPS_PER_B:
+                    quantise_h(r // GROUPS_PER_B + 1)
+                if r + 1 < GROUPS:
+                    turn_back(r + 1)
+                if r + 2 < GROUPS:
+                    mask_out(r + 2)
+                if r + 3 < GROUPS:
+                    multiply(r + 3)
                 for i in on_gpsimd(r - 1):
                     sum_second_moment(i)
+                for i in range(max(first - GROUP, 2), first):
+                    if i not in on_gpsimd(r - 1):
+                        second_moment(i)
+                if GROUPS - 3 <= r < GROUPS - 1:
+                    copy_x_to_psum(r + 1)
+                if r == 1:
+                    regroup_h_on_vector(3)
                 for k in range(GROUP):
-                    if first - GROUP + k not in on_gpsimd(r - 1):
-                        second_moment(first - GROUP + k)
-            if GROUPS - 3 <= r < GROUPS - 1:
-                copy_x_to_psum(r + 1)
-            if r % GROUPS_PER_B == 1 and r // GROUPS_PER_B + 2 < B:
-                regroup_h_on_vector(r // GROUPS_PER_B + 2)
-            for k in range(GROUP):
-                first_moment(first + k)
-            for i in on_gpsimd(r):
-                second_moment_on_gpsimd(i)
+                    first_moment(first + k)
+                for i in on_gpsimd(r):
+                    second_moment_on_gpsimd(i)
 
         def by_utterance(t):
             return t[:].rearrange("p (b j) -> p b j", b=B)

@@ -346,29 +346,28 @@ def tile_attentivestatspool_pb_kernel(tc, h, x, mask, w2, b2, g2, be2, out):
                 maximum(first + k)
                 exponentials(first + k)
             if r == 0:
-                copy_w_pair(3, on_vector=True)
-                quantise_w_pair(3)
-                multiply(1)
-                mask_out(1)
                 turn_w_pair(4)
                 turn_w_pair(5)
-                turn_back(1)
+                copy_w_pair(3, on_vector=True)
+                quantise_w_pair(3)
                 copy_w_pair(4)
                 copy_w_pair(5)
+                multiply(1)
+                mask_out(1)
                 first_moment(0)
                 first_moment(1)
+                quantise_w_pair(4)
+                quantise_w_pair(5)
+                multiply(2)
+                mask_out(2)
+                turn_back(1)
                 regroup_h_on_vector(2)
                 second_moment(0)
                 second_moment(1)
-                quantise_w_pair(4)
-                quantise_w_pair(5)
                 first_moment(2)
                 first_moment(3)
                 second_moment_on_gpsimd(2)
                 second_moment_on_gpsimd(3)
-                pass
-                multiply(2)
-                mask_out(2)
                 multiply(3)
             else:
                 if r % GROUPS_PER_B == 0 and r < GROUPS - GROUPS_PER_B:
@@ -386,7 +385,7 @@ def tile_attentivestatspool_pb_kernel(tc, h, x, mask, w2, b2, g2, be2, out):
                         second_moment(i)
                 if GROUPS - 3 <= r < GROUPS - 1:
                     copy_x_to_psum(r + 1)
-                if r == 1:
+                if r == 4:
                     regroup_h_on_vector(3)
                 for k in range(GROUP):
                     first_moment(first + k)

@@ -95,8 +95,8 @@ def tile_attentivestatspool_pb_kernel(tc, h, x, mask, w2, b2, g2, be2, out):
         load_h(1)
         load_w(6, 2)
         load_w(8, 4)
-        load_x(0)
         load_h(2)
+        load_x(0)
         load_h(3)
         load_x(1)
         load_x(2)
@@ -122,6 +122,16 @@ def tile_attentivestatspool_pb_kernel(tc, h, x, mask, w2, b2, g2, be2, out):
         def regroup_h_on_scalar(b, ts=slice(0, T)):
             nc.scalar.copy(
                 out=h_grouped[:, b, ts, :], in_=h_raw[:, b, :, ts].rearrange("p v t -> p t v")
+            )
+
+        def regroup_h_on_gpsimd(b, after):
+            nc.gpsimd.tensor_scalar(
+                out=h_grouped[:, b],
+                in0=h_raw[:, b].rearrange("p v t -> p t v"),
+                scalar1=1.0,
+                scalar2=after,
+                op0=ALU.mult,
+                op1=ALU.add,
             )
 
         def quantise_h(b, ts=slice(0, T)):
@@ -331,6 +341,9 @@ def tile_attentivestatspool_pb_kernel(tc, h, x, mask, w2, b2, g2, be2, out):
         regroup_h_on_vector(1)
         quantise_h(1)
         quantise_w_pair(2)
+        go = keep.tile([P, 1], F32)
+        nc.vector.memset(go[:], 0.0)
+        regroup_h_on_gpsimd(2, go[:])
 
         def on_gpsimd(g):
             first = g * GROUP
@@ -361,7 +374,7 @@ def tile_attentivestatspool_pb_kernel(tc, h, x, mask, w2, b2, g2, be2, out):
                 multiply(2)
                 mask_out(2)
                 turn_back(1)
-                regroup_h_on_vector(2)
+                regroup_h_on_vector(3)
                 second_moment(0)
                 second_moment(1)
                 first_moment(2)
@@ -385,8 +398,6 @@ def tile_attentivestatspool_pb_kernel(tc, h, x, mask, w2, b2, g2, be2, out):
                         second_moment(i)
                 if GROUPS - 3 <= r < GROUPS - 1:
                     copy_x_to_psum(r + 1)
-                if r == 4:
-                    regroup_h_on_vector(3)
                 for k in range(GROUP):
                     first_moment(first + k)
                 for i in on_gpsimd(r):

@@ -38,9 +38,9 @@ def tile_attentivestatspool_pb_kernel(tc, h, x, mask, w2, b2, g2, be2, out):
         keep = ctx.enter_context(tc.tile_pool(name="keep", bufs=1))
         masked_pool = ctx.enter_context(tc.tile_pool(name="masked_pool", bufs=3))
         e_pool = ctx.enter_context(tc.tile_pool(name="e_pool", bufs=6))
-        ex_pool = ctx.enter_context(tc.tile_pool(name="ex_pool", bufs=8))
+        ex_pool = ctx.enter_context(tc.tile_pool(name="ex_pool", bufs=4))
         junk_pool = ctx.enter_context(tc.tile_pool(name="junk_pool", bufs=2))
-        exx_pool = ctx.enter_context(tc.tile_pool(name="exx_pool", bufs=4))
+        exx_pool = ctx.enter_context(tc.tile_pool(name="exx_pool", bufs=3))
         psum_t = ctx.enter_context(tc.psum_pool(name="psum_t", bufs=4))
         psum_c = ctx.enter_context(tc.psum_pool(name="psum_c", bufs=4))
 
@@ -176,6 +176,7 @@ def tile_attentivestatspool_pb_kernel(tc, h, x, mask, w2, b2, g2, be2, out):
         logits_of = {}
         e_of = {}
         ex_of = {}
+        ex_pair_of = {}
         exx_of = {}
         x_of = {}
 
@@ -279,9 +280,12 @@ def tile_attentivestatspool_pb_kernel(tc, h, x, mask, w2, b2, g2, be2, out):
             e_of[i] = e
 
         def first_moment(i):
-            ex = ex_pool.tile([P, T], F32)
+            if i % 2 == 0:
+                ex_pair = ex_pool.tile([P, 2, T], F32)
+                ex_pair_of[i // 2] = ex_pair
+            ex = ex_pair_of[i // 2][:, i % 2, :]
             nc.vector.scalar_tensor_tensor(
-                out=ex[:],
+                out=ex,
                 in0=e_of[i][:],
                 scalar=1.0,
                 in1=x_for_vector(i),
@@ -295,7 +299,7 @@ def tile_attentivestatspool_pb_kernel(tc, h, x, mask, w2, b2, g2, be2, out):
             exx = junk_pool.tile([P, T], F32)
             nc.vector.scalar_tensor_tensor(
                 out=exx[:],
-                in0=ex_of[i][:],
+                in0=ex_of[i],
                 scalar=1.0,
                 in1=x_for_vector(i),
                 op0=ALU.mult,
@@ -303,15 +307,21 @@ def tile_attentivestatspool_pb_kernel(tc, h, x, mask, w2, b2, g2, be2, out):
                 accum_out=sum_exx[:, i : i + 1],
             )
 
-        def second_moment_on_gpsimd(i):
-            b, j = divmod(i, CT)
-            exx = exx_pool.tile([P, T], F32)
-            nc.gpsimd.tensor_tensor(out=exx[:], in0=ex_of[i][:], in1=x_sb[:, b, j, :], op=ALU.mult)
-            exx_of[i] = exx
+        def second_moments_on_gpsimd(first, tiles):
+            b, j = divmod(first, CT)
+            exx = exx_pool.tile([P, 2, T], F32)
+            nc.gpsimd.tensor_tensor(
+                out=exx[:, 0:tiles, :],
+                in0=ex_pair_of[first // 2][:, 0:tiles, :],
+                in1=x_sb[:, b, j : j + tiles, :],
+                op=ALU.mult,
+            )
+            for k in range(tiles):
+                exx_of[first + k] = exx[:, k, :]
 
         def sum_second_moment(i):
             nc.scalar.activation(
-                out=exx_of[i][:], in_=exx_of[i][:], func=ACT.Copy, accum_out=sum_exx[:, i : i + 1]
+                out=exx_of[i], in_=exx_of[i], func=ACT.Copy, accum_out=sum_exx[:, i : i + 1]
             )
 
         turn_w_pair(0)
@@ -379,8 +389,7 @@ def tile_attentivestatspool_pb_kernel(tc, h, x, mask, w2, b2, g2, be2, out):
                 second_moment(1)
                 first_moment(2)
                 first_moment(3)
-                second_moment_on_gpsimd(2)
-                second_moment_on_gpsimd(3)
+                second_moments_on_gpsimd(2, 2)
                 multiply(3)
             else:
                 if r % GROUPS_PER_B == 0 and r < GROUPS - GROUPS_PER_B:
@@ -401,7 +410,8 @@ def tile_attentivestatspool_pb_kernel(tc, h, x, mask, w2, b2, g2, be2, out):
                 for k in range(GROUP):
                     first_moment(first + k)
                 for i in on_gpsimd(r):
-                    second_moment_on_gpsimd(i)
+                    if i % 2 == 0:
+                        second_moments_on_gpsimd(i, 2 if i + 1 in on_gpsimd(r) else 1)
 
         def by_utterance(t):
             return t[:].rearrange("p (b j) -> p b j", b=B)

@@ -280,7 +280,7 @@ def tile_attentivestatspool_pb_kernel(tc, h, x, mask, w2, b2, g2, be2, out):
             e_of[i] = e
 
         def first_moment(i):
-            if i % 2 == 0:
+            if i // 2 not in ex_pair_of:
                 ex_pair = ex_pool.tile([P, 2, T], F32)
                 ex_pair_of[i // 2] = ex_pair
             ex = ex_pair_of[i // 2][:, i % 2, :]
@@ -386,9 +386,9 @@ def tile_attentivestatspool_pb_kernel(tc, h, x, mask, w2, b2, g2, be2, out):
                 turn_back(1)
                 regroup_h_on_vector(3)
                 second_moment(0)
-                second_moment(1)
                 first_moment(2)
                 first_moment(3)
+                second_moment(1)
                 second_moments_on_gpsimd(2, 2)
                 multiply(3)
             else:
@@ -407,7 +407,7 @@ def tile_attentivestatspool_pb_kernel(tc, h, x, mask, w2, b2, g2, be2, out):
                         second_moment(i)
                 if GROUPS - 3 <= r < GROUPS - 1:
                     copy_x_to_psum(r + 1)
-                for k in range(GROUP):
+                for k in (0, 2, 3, 1):
                     first_moment(first + k)
                 for i in on_gpsimd(r):
                     if i % 2 == 0:
@@ -487,8 +487,15 @@ def tile_attentivestatspool_pb_kernel(tc, h, x, mask, w2, b2, g2, be2, out):
         )
         nc.vector.tensor_add(out=centred[:], in0=centred[:], in1=scaled[:])
         nc.vector.reciprocal(out=spread[:], in_=spread[:])
-        nc.vector.tensor_mul(out=centred[:], in0=centred[:], in1=along_entries(spread[:]))
-        nc.vector.tensor_add(out=centred[:], in0=centred[:], in1=along_utterances(shift))
+        for b in range(B):
+            nc.vector.scalar_tensor_tensor(
+                out=centred[:, b, :],
+                in0=centred[:, b, :],
+                scalar=spread[:, b : b + 1],
+                in1=shift[:].rearrange("m s q -> m (s q)"),
+                op0=ALU.mult,
+                op1=ALU.add,
+            )
 
         nc.sync.dma_start(
             out=out.rearrange("b (s m q) o -> m (b s) (q o)", s=2, q=2 * CT),

@@ -83,10 +83,8 @@ def tile_attentivestatspool_pb_kernel(tc, h, x, mask, w2, b2, g2, be2, out):
                 nc.sync.dma_start(out=x_sb[:, b, js, :], in_=x_view[b][:, js, :])
 
         nc.vector.memset(mask_rows[:], 0.0)
-        first_half, second_half = slice(0, T // 2), slice(T // 2, T)
-        load_h(0, first_half)
+        load_h(0)
         load_w(0, 2)
-        load_h(0, second_half)
         load_w(2, 2)
         nc.sync.dma_start(
             out=mask_rows[0 : B * FT, :], in_=mask.rearrange("b o (f t) -> (b o f) t", t=P)
@@ -94,8 +92,8 @@ def tile_attentivestatspool_pb_kernel(tc, h, x, mask, w2, b2, g2, be2, out):
         load_w(4, 2)
         load_h(1)
         load_w(6, 2)
-        load_w(8, 4)
         load_h(2)
+        load_w(8, 4)
         load_x(0)
         load_h(3)
         load_x(1)
@@ -328,14 +326,12 @@ def tile_attentivestatspool_pb_kernel(tc, h, x, mask, w2, b2, g2, be2, out):
         turn_w_pair(1)
         copy_w_pair(0)
         copy_w_pair(1)
-        regroup_h_on_vector(0, first_half)
-        quantise_h(0, first_half)
-        regroup_h_on_vector(0, second_half)
+        regroup_h_on_vector(0)
+        quantise_h(0)
         nc.vector.tensor_scalar(
             out=bias_rows[:], in0=mask_rows[:], scalar1=-1.0, scalar2=MASKED, op0=ALU.add, op1=ALU.mult
         )
         quantise_w_pair(0)
-        quantise_h(0, second_half)
         bias_turned = psum_t.tile([P, P], F32, tag="logits_t")
         nc.tensor.transpose(bias_turned[:], bias_rows[:], ident[:])
         nc.vector.tensor_copy(out=mask_bias[:], in_=bias_turned[:, 0 : B * FT])

from contextlib import ExitStack

import concourse.mybir as mybir
from concourse.masks import make_identity

F32 = mybir.dt.float32
BF16 = mybir.dt.bfloat16
U32 = mybir.dt.uint32
U8 = mybir.dt.uint8
FP8X4 = mybir.dt.float8_e4m3fn_x4
ALU = mybir.AluOpType
ACT = mybir.ActivationFunctionType
AXIS = mybir.AxisListType

P = 128
PACK = 4
B, C, T, H = 4, 1536, 512, 512
CT = C // P
FT = T // P
WIDE = 512
GROUP = WIDE // P
TILES = B * CT
GROUPS = TILES // GROUP
GROUPS_PER_B = CT // GROUP
W_PAIRS = CT // 2
LOAD_PARTS = 3
EPS_STD = 1e-5
EPS_LN = 1e-5
MASKED = 1e30

FLOPS = 2 * B * C * H * T


def tile_attentivestatspool_pb_kernel(tc, h, x, mask, w2, b2, g2, be2, out):
    nc = tc.nc
    with ExitStack() as ctx:
        ctx.enter_context(tc.manual_schedule())
        keep = ctx.enter_context(tc.tile_pool(name="keep", bufs=1))
        masked_pool = ctx.enter_context(tc.tile_pool(name="masked_pool", bufs=3))
        e_pool = ctx.enter_context(tc.tile_pool(name="e_pool", bufs=6))
        ex_pool = ctx.enter_context(tc.tile_pool(name="ex_pool", bufs=4))
        junk_pool = ctx.enter_context(tc.tile_pool(name="junk_pool", bufs=2))
        exx_pool = ctx.enter_context(tc.tile_pool(name="exx_pool", bufs=3))
        psum_t = ctx.enter_context(tc.psum_pool(name="psum_t", bufs=4))
        psum_c = ctx.enter_context(tc.psum_pool(name="psum_c", bufs=4))

        ident = keep.tile([P, P], F32)
        make_identity(nc, ident[:])
        ident_bf16 = keep.tile([P, P], BF16)
        nc.vector.tensor_copy(out=ident_bf16[:], in_=ident[:])
        evens_odds = keep.tile([P, 3, P // 2], F32)
        for part in range(3):
            nc.vector.tensor_copy(out=evens_odds[:, part, :], in_=ident[:, part % 2 : P : 2])
        ones = keep.tile([P, P], F32)
        nc.vector.memset(ones[:], 1.0)
        warm_in = keep.tile([P, 1], F32)
        warm_out = keep.tile([P, 1], F32)
        nc.vector.memset(warm_in[:], 0.0)
        nc.scalar.activation(out=warm_out[:], in_=warm_in[:], func=ACT.Exp)

        mask_rows = keep.tile([P, P], BF16)
        h_raw = keep.tile([P, B, PACK, T], BF16)
        w_raw = keep.tile([P, CT * H], BF16)
        x_sb = keep.tile([P, B, CT, T], BF16)
        gain = keep.tile([P // 2, 2, 2 * CT], BF16)
        shift = keep.tile([P // 2, 2, 2 * CT], BF16)

        h_view = h.rearrange("b (p v) t -> b p v t", v=PACK)
        w_view = w2.rearrange("(p j) k -> p (j k)", j=CT)
        x_view = x.rearrange("b (p j) t -> b p j t", j=CT)
        per_part = CT // LOAD_PARTS

        def load_w(first_tile, tiles):
            ks = slice(first_tile * H, (first_tile + tiles) * H)
            nc.sync.dma_start(out=w_raw[:, ks], in_=w_view[:, ks])

        def load_h(b, ts=slice(0, T)):
            nc.sync.dma_start(out=h_raw[:, b, :, ts], in_=h_view[b][:, :, ts])

        def load_x(b):
            for part in range(LOAD_PARTS):
                js = slice(part * per_part, (part + 1) * per_part)
                nc.sync.dma_start(out=x_sb[:, b, js, :], in_=x_view[b][:, js, :])

        nc.vector.memset(mask_rows[:], 0.0)
        load_h(0)
        load_w(0, 2)
        load_w(2, 2)
        nc.sync.dma_start(
            out=mask_rows[0 : B * FT, :], in_=mask.rearrange("b o (f t) -> (b o f) t", t=P)
        )
        load_w(4, 2)
        load_h(1)
        load_w(6, 2)
        load_h(2)
        load_w(8, 4)
        load_x(0)
        load_h(3)
        load_x(1)
        load_x(2)
        load_x(3)
        nc.scalar.dma_start(out=gain[:], in_=g2.rearrange("(s m q) -> m s q", s=2, q=2 * CT))
        nc.scalar.dma_start(out=shift[:], in_=be2.rearrange("(s m q) -> m s q", s=2, q=2 * CT))

        bias_rows = keep.tile([P, P], F32)
        mask_bias = keep.tile([P, B * FT], F32)

        h_grouped = keep.tile([P, B, T, PACK], BF16, align_bytes=64)
        h_codes = keep.tile([P, B, T], U32, align_bytes=64)
        h_scales = keep.tile([P, B, T], U8, align_bytes=64)
        w_grouped = keep.tile([P, C * PACK], BF16, align_bytes=64)
        w_codes = keep.tile([P, C], U32, align_bytes=64)
        w_scales = keep.tile([P, C], U8, align_bytes=64)

        def regroup_h_on_vector(b, ts=slice(0, T)):
            nc.vector.tensor_copy(
                out=h_grouped[:, b, ts, :], in_=h_raw[:, b, :, ts].rearrange("p v t -> p t v")
            )

        def regroup_h_on_scalar(b, ts=slice(0, T)):
            nc.scalar.copy(
                out=h_grouped[:, b, ts, :], in_=h_raw[:, b, :, ts].rearrange("p v t -> p t v")
            )

        def regroup_h_on_gpsimd(b, after):
            nc.gpsimd.tensor_scalar(
                out=h_grouped[:, b],
                in0=h_raw[:, b].rearrange("p v t -> p t v"),
                scalar1=1.0,
                scalar2=after,
                op0=ALU.mult,
                op1=ALU.add,
            )

        def quantise_h(b, ts=slice(0, T)):
            nc.vector.quantize_mx(
                out=h_codes[:, b, ts].bitcast(FP8X4),
                scales=h_scales[:, b, ts],
                in_=h_grouped[:, b, ts, :].rearrange("p t v -> p (t v)"),
            )

        w_words = w_raw[:].bitcast(F32).rearrange("p (j q u) -> p j u q", j=CT, u=2)
        w_grouped_words = w_grouped[:].bitcast(F32).rearrange("p (j c u) -> p j c u", j=CT, u=2)
        turned_of = {}

        def turn_w_pair(pair):
            turned = psum_c.tile([P, 2, 2, P], F32, tag="logits_c")
            for jj in range(2):
                for u in range(2):
                    nc.tensor.transpose(turned[:, jj, u, :], w_words[:, 2 * pair + jj, u, :], ident[:])
            turned_of[pair] = turned

        def copy_w_pair(pair, on_vector=False):
            copy = nc.vector.tensor_copy if on_vector else nc.scalar.copy
            copy(
                out=w_grouped_words[:, 2 * pair : 2 * pair + 2, :, :],
                in_=turned_of[pair][:].rearrange("p j u c -> p j c u"),
            )

        def quantise_w_pair(pair):
            cs = slice(2 * pair * P, (2 * pair + 2) * P)
            nc.vector.quantize_mx(
                out=w_codes[:, cs].bitcast(FP8X4),
                scales=w_scales[:, cs],
                in_=w_grouped[:, 2 * pair * P * PACK : (2 * pair + 2) * P * PACK],
            )

        neg_max = keep.tile([P, TILES], F32)
        sum_e = keep.tile([P, TILES], F32)
        sum_ex = keep.tile([P, TILES], F32)
        sum_exx = keep.tile([P, TILES], F32)
        logits_t_of = {}
        masked_t_of = {}
        logits_of = {}
        e_of = {}
        ex_of = {}
        ex_pair_of = {}
        exx_of = {}
        x_of = {}

        def multiply(g):
            b, cg = divmod(g, GROUPS_PER_B)
            for f in range(FT):
                logits_t = psum_t.tile([P, WIDE], F32, tag="logits_t")
                nc.tensor.matmul_mx(
                    out=logits_t[:],
                    lhsT=h_codes[:, b, f * P : (f + 1) * P].bitcast(FP8X4),
                    lhsT_scale=h_scales[:, b, f * P : (f + 1) * P],
                    rhs=w_codes[:, cg * WIDE : (cg + 1) * WIDE].bitcast(FP8X4),
                    rhs_scale=w_scales[:, cg * WIDE : (cg + 1) * WIDE],
                    start=True,
                    stop=True,
                )
                logits_t_of[(g, f)] = logits_t

        def mask_out(g):
            b = g // GROUPS_PER_B
            masked_t = masked_pool.tile([P, FT, WIDE], F32)
            masked_t_of[g] = masked_t
            for f in range(FT):
                nc.scalar.activation(
                    out=masked_t[:, f, :],
                    in_=logits_t_of[(g, f)][:],
                    func=ACT.Identity,
                    bias=mask_bias[:, b * FT + f : b * FT + f + 1],
                    scale=1.0,
                )

        def multiply_pair(pair):
            cs = slice(2 * pair * P, (2 * pair + 2) * P)
            for half in range(2):
                bank = psum_t.tile([P, 2, 2 * P], F32, tag="logits_t")
                for s in range(2):
                    fs = slice((2 * half + s) * P, (2 * half + s + 1) * P)
                    nc.tensor.matmul_mx(
                        out=bank[:, s, :],
                        lhsT=h_codes[:, 0, fs].bitcast(FP8X4),
                        lhsT_scale=h_scales[:, 0, fs],
                        rhs=w_codes[:, cs].bitcast(FP8X4),
                        rhs_scale=w_scales[:, cs],
                        start=True,
                        stop=True,
                    )
                logits_t_of[(pair, half)] = bank

        def mask_out_pair(pair):
            if pair == 0:
                masked_t = masked_pool.tile([P, FT, WIDE], F32)
                masked_t_of[0] = masked_t
            for f in range(FT):
                nc.scalar.activation(
                    out=masked_t_of[0][:, f, 2 * pair * P : (2 * pair + 2) * P],
                    in_=logits_t_of[(pair, f // 2)][:, f % 2, :],
                    func=ACT.Identity,
                    bias=mask_bias[:, f : f + 1],
                    scale=1.0,
                )

        def turn_back(g, tiles=range(GROUP)):
            for jj in tiles:
                logits = psum_c.tile([P, T], F32, tag="logits_c")
                for f in range(FT):
                    nc.tensor.transpose(
                        logits[:, f * P : (f + 1) * P],
                        masked_t_of[g][:, f, jj * P : (jj + 1) * P],
                        ident[:],
                    )
                logits_of[g * GROUP + jj] = logits

        def copy_x_to_psum(g):
            for i in range(g * GROUP, (g + 1) * GROUP):
                b, j = divmod(i, CT)
                bank = psum_t.tile([P, T], BF16, tag="logits_t")
                nc.tensor.matmul(
                    out=bank[:], lhsT=ident_bf16[:], rhs=x_sb[:, b, j, :], start=True, stop=True
                )
                x_of[i] = bank[:]

        def x_for_vector(i):
            b, j = divmod(i, CT)
            return x_of.get(i, x_sb[:, b, j, :])

        def maximum(i):
            nc.vector.tensor_reduce(
                out=neg_max[:, i : i + 1], in_=logits_of[i][:], axis=AXIS.X, op=ALU.max, negate=True
            )

        def exponentials(i):
            e = e_pool.tile([P, T], F32)
            nc.scalar.activation(
                out=e[:],
                in_=logits_of[i][:],
                func=ACT.Exp,
                bias=neg_max[:, i : i + 1],
                scale=1.0,
                accum_out=sum_e[:, i : i + 1],
            )
            e_of[i] = e

        def first_moment(i):
            if i // 2 not in ex_pair_of:
                ex_pair = ex_pool.tile([P, 2, T], F32)
                ex_pair_of[i // 2] = ex_pair
            ex = ex_pair_of[i // 2][:, i % 2, :]
            nc.vector.scalar_tensor_tensor(
                out=ex,
                in0=e_of[i][:],
                scalar=1.0,
                in1=x_for_vector(i),
                op0=ALU.mult,
                op1=ALU.mult,
                accum_out=sum_ex[:, i : i + 1],
            )
            ex_of[i] = ex

        def second_moment(i):
            exx = junk_pool.tile([P, T], F32)
            nc.vector.scalar_tensor_tensor(
                out=exx[:],
                in0=ex_of[i],
                scalar=1.0,
                in1=x_for_vector(i),
                op0=ALU.mult,
                op1=ALU.mult,
                accum_out=sum_exx[:, i : i + 1],
            )

        def second_moments_on_gpsimd(first, tiles):
            b, j = divmod(first, CT)
            exx = exx_pool.tile([P, 2, T], F32)
            nc.gpsimd.tensor_tensor(
                out=exx[:, 0:tiles, :],
                in0=ex_pair_of[first // 2][:, 0:tiles, :],
                in1=x_sb[:, b, j : j + tiles, :],
                op=ALU.mult,
            )
            for k in range(tiles):
                exx_of[first + k] = exx[:, k, :]

        def sum_second_moment(i):
            nc.scalar.activation(
                out=exx_of[i], in_=exx_of[i], func=ACT.Copy, accum_out=sum_exx[:, i : i + 1]
            )

        turn_w_pair(0)
        turn_w_pair(1)
        copy_w_pair(0)
        copy_w_pair(1)
        regroup_h_on_vector(0)
        quantise_h(0)
        nc.vector.tensor_scalar(
            out=bias_rows[:], in0=mask_rows[:], scalar1=-1.0, scalar2=MASKED, op0=ALU.add, op1=ALU.mult
        )
        quantise_w_pair(0)
        bias_turned = psum_t.tile([P, P], F32, tag="logits_t")
        nc.tensor.transpose(bias_turned[:], bias_rows[:], ident[:])
        nc.vector.tensor_copy(out=mask_bias[:], in_=bias_turned[:, 0 : B * FT])
        quantise_w_pair(1)
        turn_w_pair(2)
        copy_w_pair(2)
        multiply_pair(0)
        mask_out_pair(0)
        multiply_pair(1)
        mask_out_pair(1)
        turn_back(0)
        turn_w_pair(3)
        regroup_h_on_vector(1)
        quantise_h(1)
        quantise_w_pair(2)
        go = keep.tile([P, 1], F32)
        nc.vector.memset(go[:], 0.0)
        regroup_h_on_gpsimd(2, go[:])

        def on_gpsimd(g):
            first = g * GROUP
            if g == GROUPS - 1:
                return (first,)
            if g >= GROUPS - 3:
                return (first + 2, first + 3, first, first + 1)
            return (first + 2, first + 3)

        for r in range(GROUPS):
            first = r * GROUP
            for k in range(GROUP):
                maximum(first + k)
                exponentials(first + k)
            if r == 0:
                turn_w_pair(4)
                turn_w_pair(5)
                copy_w_pair(3, on_vector=True)
                quantise_w_pair(3)
                copy_w_pair(4)
                copy_w_pair(5)
                multiply(1)
                mask_out(1)
                first_moment(0)
                first_moment(1)
                quantise_w_pair(4)
                quantise_w_pair(5)
                multiply(2)
                mask_out(2)
                turn_back(1)
                regroup_h_on_vector(3)
                second_moment(0)
                first_moment(2)
                first_moment(3)
                second_moment(1)
                second_moments_on_gpsimd(2, 2)
                multiply(3)
            else:
                if r % GROUPS_PER_B == 0 and r < GROUPS - GROUPS_PER_B:
                    quantise_h(r // GROUPS_PER_B + 1)
                if r + 1 < GROUPS:
                    turn_back(r + 1)
                if r + 2 < GROUPS:
                    mask_out(r + 2)
                if r + 3 < GROUPS:
                    multiply(r + 3)
                for i in on_gpsimd(r - 1):
                    sum_second_moment(i)
                for i in range(max(first - GROUP, 2), first):
                    if i not in on_gpsimd(r - 1):
                        second_moment(i)
                if GROUPS - 3 <= r < GROUPS - 1:
                    copy_x_to_psum(r + 1)
                for k in (0, 2, 3, 1):
                    first_moment(first + k)
                for i in on_gpsimd(r):
                    if i % 2 == 0:
                        second_moments_on_gpsimd(i, 2 if i + 1 in on_gpsimd(r) else 1)

        def by_utterance(t):
            return t[:].rearrange("p (b j) -> p b j", b=B)

        stats = keep.tile([P, B, 2, CT], F32)
        squares = keep.tile([P, B, 2, CT], F32)
        inv_e = keep.tile([P, TILES], F32)
        sum_second_moment(TILES - GROUP)
        second_moment(TILES - GROUP + 1)
        nc.vector.reciprocal(out=inv_e[:], in_=sum_e[:])
        nc.vector.tensor_mul(out=stats[:, :, 0, :], in0=by_utterance(sum_ex), in1=by_utterance(inv_e))
        second_moment(TILES - GROUP + 2)
        nc.vector.tensor_mul(out=squares[:, :, 0, :], in0=stats[:, :, 0, :], in1=stats[:, :, 0, :])
        second_moment(TILES - GROUP + 3)
        nc.scalar.activation(out=warm_out[:], in_=warm_in[:], func=ACT.Sqrt)

        entries = 2 * C
        width = 2 * CT
        rows = keep.tile([P, 2 * B], F32)
        second = keep.tile([P, B, CT], F32)
        flat = stats[:].rearrange("p b s j -> p b (s j)")

        half = P // 2
        pair_width = 2 * width

        def along_entries(t):
            return t.unsqueeze(2).to_broadcast([half, B, pair_width])

        def along_utterances(t):
            return t[:].rearrange("m s q -> m (s q)").unsqueeze(1).to_broadcast([half, B, pair_width])

        nc.vector.tensor_mul(out=second[:], in0=by_utterance(sum_exx), in1=by_utterance(inv_e))
        nc.vector.tensor_sub(out=second[:], in0=second[:], in1=squares[:, :, 0, :])
        nc.vector.tensor_scalar_max(out=squares[:, :, 1, :], in0=second[:], scalar1=EPS_STD)
        nc.scalar.activation(out=stats[:, :, 1, :], in_=squares[:, :, 1, :], func=ACT.Sqrt)
        nc.vector.tensor_reduce(
            out=rows[:, B : 2 * B], in_=squares[:].rearrange("p b s j -> p b (s j)"), axis=AXIS.X, op=ALU.add
        )
        nc.vector.tensor_reduce(out=rows[:, 0:B], in_=flat, axis=AXIS.X, op=ALU.add)

        totals = psum_t.tile([P, 2 * B], F32, tag="logits_t")
        nc.tensor.matmul(out=totals[:], lhsT=ones[:], rhs=rows[:], start=True, stop=True)
        merged = psum_t.tile([P, 2 * B, 2, CT], F32, tag="logits_t")
        for r in range(2):
            nc.tensor.matmul(
                out=merged[:, :, r, :],
                lhsT=evens_odds[:].rearrange("p a m -> p (a m)")[:, r * half : r * half + P],
                rhs=stats[:].rearrange("p b s j -> p (b s j)"),
                start=True,
                stop=True,
            )
        scaled = keep.tile([half, B, pair_width], F32)
        neg_mu = keep.tile([half, B], F32)
        spread = keep.tile([half, B], F32)
        centred = keep.tile([half, B, pair_width], F32)
        totals = totals[0:half, :]
        nc.vector.tensor_scalar_mul(out=neg_mu[:], in0=totals[:, 0:B], scalar1=-1.0 / entries)
        nc.vector.tensor_mul(out=spread[:], in0=neg_mu[:], in1=totals[:, 0:B])
        nc.vector.scalar_tensor_tensor(
            out=spread[:],
            in0=spread[:],
            scalar=entries * EPS_LN,
            in1=totals[:, B : 2 * B],
            op0=ALU.add,
            op1=ALU.add,
        )
        nc.scalar.activation(out=spread[:], in_=spread[:], func=ACT.Sqrt, scale=1.0 / entries)
        nc.vector.tensor_mul(out=centred[:], in0=along_utterances(gain), in1=along_entries(neg_mu[:]))
        nc.vector.tensor_mul(
            out=scaled[:],
            in0=merged[0:half, :, :, :].rearrange("m (b s) r j -> m b (s r j)", b=B),
            in1=along_utterances(gain),
        )
        nc.vector.tensor_add(out=centred[:], in0=centred[:], in1=scaled[:])
        nc.vector.reciprocal(out=spread[:], in_=spread[:])
        for b in range(B):
            nc.vector.scalar_tensor_tensor(
                out=centred[:, b, :],
                in0=centred[:, b, :],
                scalar=spread[:, b : b + 1],
                in1=shift[:].rearrange("m s q -> m (s q)"),
                op0=ALU.mult,
                op1=ALU.add,
            )

        nc.sync.dma_start(
            out=out.rearrange("b (s m q) o -> m (b s) (q o)", s=2, q=2 * CT),
            in_=centred[:].rearrange("m b (s q) -> m (b s) q", s=2),
        )
